import numpy as np
import ml_dtypes


def mxq(x, axis, fmt="e4m3"):
    dtype, down = {"e4m3": (ml_dtypes.float8_e4m3fn, 7), "e5m2": (ml_dtypes.float8_e5m2, 14)}[fmt]
    v = np.moveaxis(np.asarray(x, np.float32).astype(ml_dtypes.bfloat16).astype(np.float64), axis, -1)
    blocks = v.reshape(v.shape[:-1] + (-1, 32))
    amax = np.abs(blocks).max(-1, keepdims=True)
    byte = np.maximum(np.where(amax > 0, np.frexp(amax)[1] - 1 + 127, 0) - down, 1)
    scale = np.exp2(byte - 127.0)
    codes = (blocks / scale).astype(np.float32).astype(dtype).astype(np.float64)
    return np.moveaxis((codes * scale).reshape(v.shape), -1, axis)


WIDE = False


def mx_kscale(k):
    if not WIDE:
        return np.ones(k)
    levels = np.array([10, -10, 5, -5, 0])
    a = np.random.permutation(np.resize(levels, k // 512 * 4)).reshape(k // 512, 4)
    idx = np.arange(k)
    return np.exp2(a[idx // 512, idx % 128 // 32])


BF16 = ml_dtypes.bfloat16


def bf(x):
    return np.asarray(x, np.float32).astype(BF16)


def f64(x):
    return np.asarray(x).astype(np.float64)


E2M1 = np.array([0.0, 0.5, 1.0, 1.5, 2.0, 3.0, 4.0, 6.0, -0.0, -0.5, -1.0, -1.5, -2.0, -3.0, -4.0, -6.0])


def pack_weight(w, fmt):
    k, n = w.shape
    w = f64(bf(w)).reshape(k // 32, 32, n)
    amax = np.abs(w).max(1)
    if fmt == "e4m3":
        byte = np.frexp(amax)[1] - 1 + 127 - 7
    else:
        mant, ex = np.frexp(amax / 6.0)
        byte = np.where(mant > 0.5, ex, ex - 1) + 127
    byte = np.clip(np.where(amax > 0, byte, 1), 1, 254)
    scaled = (w * np.exp2(127.0 - byte)[:, None, :]).reshape(k, n).astype(np.float32)
    by_word = np.ascontiguousarray(scaled.reshape(k // 512, 128, 4, n).transpose(0, 1, 3, 2))
    if fmt == "e4m3":
        words = by_word.astype(ml_dtypes.float8_e4m3fn).view(np.uint8)
    else:
        c = by_word.astype(ml_dtypes.float4_e2m1fn).view(np.uint8) & 0xF
        words = c[..., 0::2] | (c[..., 1::2] << 4)
    return np.ascontiguousarray(words), np.ascontiguousarray(byte.astype(np.uint8).reshape(k // 512, 16, n))


def unpack_weight(words, scales, fmt):
    g, p, n, _ = words.shape
    if fmt == "e4m3":
        vals = np.ascontiguousarray(words).view(ml_dtypes.float8_e4m3fn).astype(np.float64)
    else:
        nib = np.empty((g, p, n, 4), np.uint8)
        nib[..., 0::2] = words & 0xF
        nib[..., 1::2] = words >> 4
        vals = E2M1[nib]
    vals = vals * np.repeat(np.exp2(scales.astype(np.float64) - 127.0), 8, axis=1)[..., None]
    return vals.transpose(0, 1, 3, 2).reshape(g * 512, n)


B, N, HID, ITERS = 512, 32, 2048, 10
DOUT = N * N
SLOPE = 0.01
EPS = 1e-8
FMT = "e4m3"


def leaky(v):
    return np.where(v >= 0.0, v, SLOPE * v)


def l1_normalize(r, axis):
    return r / np.maximum(np.abs(r).sum(axis=axis, keepdims=True), EPS)


def setup_inputs():
    s, t = mx_kscale(HID), mx_kscale(HID)
    h3 = bf(leaky(np.random.standard_normal((B, HID)) * 1.1) * s)
    W4_words, W4_scales = pack_weight(np.random.standard_normal((HID, HID)) * 1.4 / np.sqrt(HID) / s[:, None] * t, FMT)
    b4 = bf(np.random.standard_normal(HID) * 0.3 * t)
    W5_words, W5_scales = pack_weight(np.random.standard_normal((HID, DOUT)) * 2.0 / np.sqrt(HID) / t[:, None], FMT)
    b5 = bf(np.random.standard_normal(DOUT) * 3.0 - 4.0)
    return {"h3": h3,
            "W4_words": W4_words,
            "W4_scales": W4_scales,
            "b4": b4,
            "W5_words": W5_words,
            "W5_scales": W5_scales,
            "b5": b5}


def reference(h3, W4_words, W4_scales, b4, W5_words, W5_scales, b5):
    h4 = leaky((mxq(f64(h3), 1, "e4m3") @ unpack_weight(W4_words, W4_scales, FMT)) + f64(b4))
    r = ((mxq(h4, 1, "e4m3") @ unpack_weight(W5_words, W5_scales, FMT)) + f64(b5)).reshape(B, N, N)
    r = np.logaddexp(r, 0.0)
    for _ in range(ITERS):
        r = l1_normalize(r, 1)
        r = l1_normalize(r, 2)
    return r

@@ -1,0 +1,209 @@
+from contextlib import ExitStack
+
+import concourse.mybir as mybir
+from concourse.masks import make_identity
+
+FLOPS = 2 * 512 * 2048 * 2048 + 2 * 512 * 2048 * 1024
+
+F32 = mybir.dt.float32
+BF16 = mybir.dt.bfloat16
+I32 = mybir.dt.int32
+U8 = mybir.dt.uint8
+FP8X4 = mybir.dt.float8_e4m3fn_x4
+ALU = mybir.AluOpType
+ACT = mybir.ActivationFunctionType
+AXIS = mybir.AxisListType
+
+P = 128
+PACK = 4
+K_PASS = P * PACK
+HID = 2048
+PASSES = HID // K_PASS
+TOKENS = 512
+TOKEN_TILES = TOKENS // P
+PAIRS = TOKEN_TILES // 2
+SIDE = 32
+DOUT = SIDE * SIDE
+N_TILE = 512
+SLOPE = 0.01
+EPS = 1e-8
+ROUNDS = 10
+
+
+def load_weight(nc, keep, words, scales, n_cols, name):
+    planes = keep.tile([P, n_cols], U8, name=name + "_planes", align_bytes=64)
+    nc.vector.memset(planes[:].bitcast(I32), 0)
+    for quadrant in range(4):
+        nc.sync.dma_start(
+            out=planes[32 * quadrant : 32 * quadrant + 16, :].bitcast(I32),
+            in_=scales[:, 4 * quadrant : 4 * quadrant + 4, :].bitcast(I32),
+        )
+    codes = keep.tile([P, PASSES, n_cols], I32, name=name + "_codes", align_bytes=64)
+    return codes, planes
+
+
+def load_weight_columns(nc, codes, words, cols):
+    by_partition = words.rearrange("g p n t -> g p (n t)").bitcast(I32).rearrange("g p n -> p g n")
+    nc.sync.dma_start(out=codes[:, :, cols], in_=by_partition[:, :, cols])
+
+
+def quantise_rows(nc, psum_t, work, ident, rows, codes, planes):
+    words = rows.bitcast(F32)
+    grouped = work.tile([P, PASSES, P, PACK], BF16, tag="grouped", align_bytes=64)
+    for g in range(PASSES):
+        flipped = psum_t.tile([P, 2, P], F32, tag="flipped")
+        for u in range(2):
+            nc.tensor.transpose(flipped[:, u, :], words[:, 256 * g + u : 256 * (g + 1) : 2], ident[:])
+        nc.scalar.copy(
+            out=grouped[:, g, :, :].rearrange("p r (u e) -> p r u e", e=2),
+            in_=flipped[:].bitcast(BF16).rearrange("p u (r e) -> p r u e", e=2),
+        )
+    nc.vector.quantize_mx(
+        out=codes.bitcast(FP8X4),
+        scales=planes,
+        in_=grouped[:].rearrange("p g r t -> p (g r t)"),
+    )
+
+
+def mx_product(nc, acc, x_codes, x_planes, w_codes, w_planes, cols):
+    for g in range(PASSES):
+        tokens = slice(g * P, (g + 1) * P)
+        nc.tensor.matmul_mx(
+            out=acc,
+            lhsT=x_codes[:, tokens].bitcast(FP8X4),
+            lhsT_scale=x_planes[:, tokens],
+            rhs=w_codes[:, g, cols].bitcast(FP8X4),
+            rhs_scale=w_planes[4 * g : P, cols],
+            start=(g == 0),
+            stop=(g == PASSES - 1),
+        )
+
+
+def scale_rows(nc, dst, src, factor):
+    for x in range(SIDE):
+        nc.scalar.activation(out=dst[:, 0, x, :], in_=src[:, 0, x, :], func=ACT.Copy, scale=factor[:, 0, x : x + 1])
+    nc.gpsimd.tensor_tensor(
+        out=dst[:, 1, :, :],
+        in0=src[:, 1, :, :],
+        in1=factor[:, 1, :].unsqueeze(2).to_broadcast([P, SIDE, SIDE]),
+        op=ALU.mult,
+    )
+
+
+def update_factor(nc, small, factor, scaled):
+    sums = small.tile([P, 2, SIDE], F32, tag="sums")
+    nc.vector.tensor_reduce(out=sums[:], in_=scaled.rearrange("p t x y -> p t y x"), axis=AXIS.X, op=ALU.add)
+    nc.vector.reciprocal(out=sums[:], in_=sums[:])
+    nc.vector.scalar_tensor_tensor(
+        out=factor[:], in0=factor[:], scalar=1.0 / EPS, in1=sums[:], op0=ALU.mult, op1=ALU.min
+    )
+
+
+def tile_matchingnet_pa_kernel(tc, h3, W4_words, W4_scales, b4, W5_words, W5_scales, b5, out):
+    nc = tc.nc
+    with ExitStack() as stack:
+        keep = stack.enter_context(tc.tile_pool(name="keep", bufs=1))
+        work = stack.enter_context(tc.tile_pool(name="work", bufs=2))
+        small = stack.enter_context(tc.tile_pool(name="small", bufs=4))
+        psum_t = stack.enter_context(tc.psum_pool(name="psum_t", bufs=2))
+        psum_acc = stack.enter_context(tc.psum_pool(name="psum_acc", bufs=6))
+
+        w4_codes, w4_planes = load_weight(nc, keep, W4_words, W4_scales, HID, "w4")
+        w5_codes, w5_planes = load_weight(nc, keep, W5_words, W5_scales, DOUT, "w5")
+        x_rows = keep.tile([P, TOKEN_TILES, HID], BF16, name="x_rows")
+        for m in range(TOKEN_TILES):
+            nc.sync.dma_start(out=x_rows[:, m, :], in_=h3[m * P : (m + 1) * P, :])
+        for c in range(HID // N_TILE):
+            load_weight_columns(nc, w4_codes, W4_words, slice(c * N_TILE, (c + 1) * N_TILE))
+        for c in range(DOUT // N_TILE):
+            load_weight_columns(nc, w5_codes, W5_words, slice(c * N_TILE, (c + 1) * N_TILE))
+        b4_all = keep.tile([P, HID], BF16, name="b4_all")
+        nc.scalar.dma_start(out=b4_all[:], in_=b4.partition_broadcast(P))
+        b5_all = keep.tile([P, DOUT], BF16, name="b5_all")
+        nc.scalar.dma_start(out=b5_all[:], in_=b5.partition_broadcast(P))
+
+        ident = keep.tile([P, P], F32, name="ident")
+        make_identity(nc, ident[:])
+        one = keep.tile([P, 1], F32, name="one")
+        nc.vector.memset(one[:], 1.0)
+
+        x_codes = keep.tile([P, TOKEN_TILES, PASSES * P], I32, name="x_codes", align_bytes=64)
+        x_planes = keep.tile([P, TOKEN_TILES, PASSES * P], U8, name="x_planes", align_bytes=64)
+        for m in range(TOKEN_TILES):
+            quantise_rows(nc, psum_t, work, ident, x_rows[:, m, :], x_codes[:, m, :], x_planes[:, m, :])
+
+        h_codes = keep.tile([P, TOKEN_TILES, PASSES * P], I32, name="h_codes", align_bytes=64)
+        h_planes = keep.tile([P, TOKEN_TILES, PASSES * P], U8, name="h_planes", align_bytes=64)
+
+        kernels = []
+        kernels_t = []
+        for pair in range(PAIRS):
+            z = work.tile([P, 2, DOUT], F32, tag="z", bufs=1)
+            for t in range(2):
+                m = 2 * pair + t
+                h4 = work.tile([P, HID], BF16, tag="h4")
+                for c in range(HID // N_TILE):
+                    cols = slice(c * N_TILE, (c + 1) * N_TILE)
+                    acc = psum_acc.tile([P, N_TILE], F32, tag="acc")
+                    mx_product(nc, acc[:], x_codes[:, m, :], x_planes[:, m, :], w4_codes, w4_planes, cols)
+                    pre = work.tile([P, N_TILE], F32, tag="pre")
+                    nc.vector.tensor_tensor(out=pre[:], in0=acc[:], in1=b4_all[:, cols], op=ALU.add)
+                    nc.vector.scalar_tensor_tensor(
+                        out=h4[:, cols], in0=pre[:], scalar=SLOPE, in1=pre[:], op0=ALU.mult, op1=ALU.max
+                    )
+                quantise_rows(nc, psum_t, work, ident, h4[:], h_codes[:, m, :], h_planes[:, m, :])
+                for c in range(DOUT // N_TILE):
+                    cols = slice(c * N_TILE, (c + 1) * N_TILE)
+                    acc = psum_acc.tile([P, N_TILE], F32, tag="acc")
+                    mx_product(nc, acc[:], h_codes[:, m, :], h_planes[:, m, :], w5_codes, w5_planes, cols)
+                    nc.vector.tensor_tensor(out=z[:, t, cols], in0=acc[:], in1=b5_all[:, cols], op=ALU.add)
+
+            tail = work.tile([P, 2, DOUT], F32, tag="tail", bufs=1)
+            nc.scalar.activation(out=tail[:], in_=z[:], func=ACT.Abs)
+            nc.scalar.activation(out=tail[:], in_=tail[:], func=ACT.Exp, scale=-1.0)
+            nc.scalar.activation(out=tail[:], in_=tail[:], func=ACT.Ln, bias=one[:])
+            ramp = work.tile([P, 2, DOUT], F32, tag="ramp", bufs=1)
+            nc.scalar.activation(out=ramp[:], in_=z[:], func=ACT.Relu)
+            kern = keep.tile([P, 2, SIDE, SIDE], F32, name="kern%d" % pair)
+            nc.gpsimd.tensor_tensor(
+                out=kern[:].rearrange("p t i j -> p t (i j)"), in0=ramp[:], in1=tail[:], op=ALU.add
+            )
+            kern_t = keep.tile([P, 2, SIDE, SIDE], F32, name="kern_t%d" % pair)
+            for t in range(2):
+                nc.gpsimd.tensor_tensor(
+                    out=kern_t[:, t, :, :],
+                    in0=ramp[:, t, :].rearrange("p (i j) -> p j i", j=SIDE),
+                    in1=tail[:, t, :].rearrange("p (i j) -> p j i", j=SIDE),
+                    op=ALU.add,
+                )
+            kernels.append(kern)
+            kernels_t.append(kern_t)
+
+        row = []
+        col = []
+        scaled = []
+        for pair in range(PAIRS):
+            row.append(keep.tile([P, 2, SIDE], F32, name="row%d" % pair))
+            col.append(keep.tile([P, 2, SIDE], F32, name="col%d" % pair))
+            scaled.append(keep.tile([P, 2, SIDE, SIDE], F32, name="scaled%d" % pair))
+            nc.vector.memset(row[pair][:], 1.0)
+            nc.vector.memset(col[pair][:], 1.0)
+        for it in range(ROUNDS):
+            for pair in range(PAIRS):
+                if it == 0:
+                    update_factor(nc, small, col[pair], kernels[pair][:])
+                else:
+                    scale_rows(nc, scaled[pair], kernels[pair], row[pair])
+                    update_factor(nc, small, col[pair], scaled[pair][:])
+            for pair in range(PAIRS):
+                scale_rows(nc, scaled[pair], kernels_t[pair], col[pair])
+                update_factor(nc, small, row[pair], scaled[pair][:])
+        for pair in range(PAIRS):
+            result = kernels[pair]
+            scale_rows(nc, result, scaled[pair][:].rearrange("p t j i -> p t i j"), row[pair])
+            for t in range(2):
+                m = 2 * pair + t
+                nc.sync.dma_start(
+                    out=out[m * P : (m + 1) * P, :, :].rearrange("b i j -> b (i j)"),
+                    in_=result[:, t, :, :].rearrange("p i j -> p (i j)"),
+                )

@@ -21,13 +21,16 @@ HID = 2048
 PASSES = HID // K_PASS
 TOKENS = 512
 TOKEN_TILES = TOKENS // P
-PAIRS = TOKEN_TILES // 2
+GROUPS = 2
+GROUP_TILES = TOKEN_TILES // GROUPS
+PIECES = 4
 SIDE = 32
 DOUT = SIDE * SIDE
 N_TILE = 512
 SLOPE = 0.01
 EPS = 1e-8
 ROUNDS = 10
+BLOCK_ROWS = P // (GROUP_TILES * SIDE)
 
 
 def load_weight(nc, keep, words, scales, n_cols, name):
@@ -79,20 +82,41 @@ def mx_product(nc, acc, x_codes, x_planes, w_codes, w_planes, cols):
         )
 
 
-def scale_rows(nc, dst, src, factor):
-    for x in range(SIDE):
-        nc.scalar.activation(out=dst[:, 0, x, :], in_=src[:, 0, x, :], func=ACT.Copy, scale=factor[:, 0, x : x + 1])
-    nc.gpsimd.tensor_tensor(
-        out=dst[:, 1, :, :],
-        in0=src[:, 1, :, :],
-        in1=factor[:, 1, :].unsqueeze(2).to_broadcast([P, SIDE, SIDE]),
-        op=ALU.mult,
+def scale_rows(nc, scaled, mat, factor):
+    step = SIDE // PIECES
+    for piece in range(PIECES):
+        rows = slice(piece * step, (piece + 1) * step)
+        nc.vector.tensor_tensor(
+            out=scaled[:, rows, :, :],
+            in0=mat[:, rows, :, :],
+            in1=factor[:, :, rows].rearrange("p t x -> p x t").unsqueeze(3).to_broadcast([P, step, GROUP_TILES, SIDE]),
+            op=ALU.mult,
+        )
+
+
+def update_factor(nc, psum_s, small, ident, factor, scaled):
+    blocks = SIDE // BLOCK_ROWS
+    across = psum_s.tile([P, P], F32, tag="across")
+    for b in range(blocks):
+        nc.tensor.matmul(
+            out=across[:],
+            lhsT=scaled[:, b * BLOCK_ROWS : (b + 1) * BLOCK_ROWS, :, :].rearrange("p x t y -> p (x t y)"),
+            rhs=ident[:],
+            is_transpose=True,
+            start=(b == 0),
+            stop=(b == blocks - 1),
+        )
+    across_sb = small.tile([P, P], F32, tag="across_sb")
+    nc.scalar.copy(out=across_sb[:], in_=across[:])
+    back = psum_s.tile([P, P], F32, tag="back")
+    nc.tensor.transpose(back[:], across_sb[:], ident[:])
+    sums = small.tile([P, GROUP_TILES, SIDE], F32, tag="sums")
+    nc.vector.tensor_reduce(
+        out=sums[:].rearrange("p t y -> p (t y)"),
+        in_=back[:].rearrange("p (x c) -> p c x", x=BLOCK_ROWS),
+        axis=AXIS.X,
+        op=ALU.add,
     )
-
-
-def update_factor(nc, small, factor, scaled):
-    sums = small.tile([P, 2, SIDE], F32, tag="sums")
-    nc.vector.tensor_reduce(out=sums[:], in_=scaled.rearrange("p t x y -> p t y x"), axis=AXIS.X, op=ALU.add)
     nc.vector.reciprocal(out=sums[:], in_=sums[:])
     nc.vector.scalar_tensor_tensor(
         out=factor[:], in0=factor[:], scalar=1.0 / EPS, in1=sums[:], op0=ALU.mult, op1=ALU.min
@@ -104,9 +128,10 @@ def tile_matchingnet_pa_kernel(tc, h3, W4_words, W4_scales, b4, W5_words, W5_sca
     with ExitStack() as stack:
         keep = stack.enter_context(tc.tile_pool(name="keep", bufs=1))
         work = stack.enter_context(tc.tile_pool(name="work", bufs=2))
-        small = stack.enter_context(tc.tile_pool(name="small", bufs=4))
+        small = stack.enter_context(tc.tile_pool(name="small", bufs=2))
         psum_t = stack.enter_context(tc.psum_pool(name="psum_t", bufs=2))
-        psum_acc = stack.enter_context(tc.psum_pool(name="psum_acc", bufs=6))
+        psum_acc = stack.enter_context(tc.psum_pool(name="psum_acc", bufs=4))
+        psum_s = stack.enter_context(tc.psum_pool(name="psum_s", bufs=1))
 
         w4_codes, w4_planes = load_weight(nc, keep, W4_words, W4_scales, HID, "w4")
         w5_codes, w5_planes = load_weight(nc, keep, W5_words, W5_scales, DOUT, "w5")
@@ -129,80 +154,87 @@ def tile_matchingnet_pa_kernel(tc, h3, W4_words, W4_scales, b4, W5_words, W5_sca
 
         x_codes = keep.tile([P, TOKEN_TILES, PASSES * P], I32, name="x_codes", align_bytes=64)
         x_planes = keep.tile([P, TOKEN_TILES, PASSES * P], U8, name="x_planes", align_bytes=64)
+        h_codes = keep.tile([P, TOKEN_TILES, PASSES * P], I32, name="h_codes", align_bytes=64)
+        h_planes = keep.tile([P, TOKEN_TILES, PASSES * P], U8, name="h_planes", align_bytes=64)
         for m in range(TOKEN_TILES):
             quantise_rows(nc, psum_t, work, ident, x_rows[:, m, :], x_codes[:, m, :], x_planes[:, m, :])
 
-        h_codes = keep.tile([P, TOKEN_TILES, PASSES * P], I32, name="h_codes", align_bytes=64)
-        h_planes = keep.tile([P, TOKEN_TILES, PASSES * P], U8, name="h_planes", align_bytes=64)
+        def layer_1(m):
+            h4 = work.tile([P, HID], BF16, tag="h4")
+            for c in range(HID // N_TILE):
+                cols = slice(c * N_TILE, (c + 1) * N_TILE)
+                acc = psum_acc.tile([P, N_TILE], F32, tag="acc")
+                mx_product(nc, acc[:], x_codes[:, m, :], x_planes[:, m, :], w4_codes, w4_planes, cols)
+                pre = work.tile([P, N_TILE], F32, tag="pre", bufs=3)
+                nc.vector.tensor_tensor(out=pre[:], in0=acc[:], in1=b4_all[:, cols], op=ALU.add)
+                low = work.tile([P, N_TILE], F32, tag="low", bufs=3)
+                nc.scalar.activation(out=low[:], in_=pre[:], func=ACT.Copy, scale=SLOPE)
+                nc.vector.tensor_tensor(out=h4[:, cols], in0=pre[:], in1=low[:], op=ALU.max)
+            return h4
 
-        kernels = []
-        kernels_t = []
-        for pair in range(PAIRS):
-            z = work.tile([P, 2, DOUT], F32, tag="z", bufs=1)
-            for t in range(2):
-                m = 2 * pair + t
-                h4 = work.tile([P, HID], BF16, tag="h4")
-                for c in range(HID // N_TILE):
-                    cols = slice(c * N_TILE, (c + 1) * N_TILE)
-                    acc = psum_acc.tile([P, N_TILE], F32, tag="acc")
-                    mx_product(nc, acc[:], x_codes[:, m, :], x_planes[:, m, :], w4_codes, w4_planes, cols)
-                    pre = work.tile([P, N_TILE], F32, tag="pre")
-                    nc.vector.tensor_tensor(out=pre[:], in0=acc[:], in1=b4_all[:, cols], op=ALU.add)
-                    nc.vector.scalar_tensor_tensor(
-                        out=h4[:, cols], in0=pre[:], scalar=SLOPE, in1=pre[:], op0=ALU.mult, op1=ALU.max
-                    )
-                quantise_rows(nc, psum_t, work, ident, h4[:], h_codes[:, m, :], h_planes[:, m, :])
-                for c in range(DOUT // N_TILE):
-                    cols = slice(c * N_TILE, (c + 1) * N_TILE)
-                    acc = psum_acc.tile([P, N_TILE], F32, tag="acc")
-                    mx_product(nc, acc[:], h_codes[:, m, :], h_planes[:, m, :], w5_codes, w5_planes, cols)
-                    nc.vector.tensor_tensor(out=z[:, t, cols], in0=acc[:], in1=b5_all[:, cols], op=ALU.add)
+        def layer_2(m, h4, z):
+            quantise_rows(nc, psum_t, work, ident, h4[:], h_codes[:, m, :], h_planes[:, m, :])
+            for c in range(DOUT // N_TILE):
+                cols = slice(c * N_TILE, (c + 1) * N_TILE)
+                acc = psum_acc.tile([P, N_TILE], F32, tag="acc")
+                mx_product(nc, acc[:], h_codes[:, m, :], h_planes[:, m, :], w5_codes, w5_planes, cols)
+                nc.vector.tensor_tensor(out=z[:, cols], in0=acc[:], in1=b5_all[:, cols], op=ALU.add)
 
-            tail = work.tile([P, 2, DOUT], F32, tag="tail", bufs=1)
+        kern = []
+        kern_t = []
+        for g in range(GROUPS):
+            z = work.tile([P, GROUP_TILES, DOUT], F32, tag="z", bufs=1)
+            first = layer_1(GROUP_TILES * g)
+            second = layer_1(GROUP_TILES * g + 1)
+            layer_2(GROUP_TILES * g, first, z[:, 0, :])
+            layer_2(GROUP_TILES * g + 1, second, z[:, 1, :])
+
+            tail = work.tile([P, GROUP_TILES, DOUT], F32, tag="tail", bufs=1)
             nc.scalar.activation(out=tail[:], in_=z[:], func=ACT.Abs)
             nc.scalar.activation(out=tail[:], in_=tail[:], func=ACT.Exp, scale=-1.0)
             nc.scalar.activation(out=tail[:], in_=tail[:], func=ACT.Ln, bias=one[:])
-            ramp = work.tile([P, 2, DOUT], F32, tag="ramp", bufs=1)
+            ramp = work.tile([P, GROUP_TILES, DOUT], F32, tag="ramp", bufs=1)
             nc.scalar.activation(out=ramp[:], in_=z[:], func=ACT.Relu)
-            kern = keep.tile([P, 2, SIDE, SIDE], F32, name="kern%d" % pair)
+            kern.append(keep.tile([P, SIDE, GROUP_TILES, SIDE], F32, name="kern%d" % g))
             nc.gpsimd.tensor_tensor(
-                out=kern[:].rearrange("p t i j -> p t (i j)"), in0=ramp[:], in1=tail[:], op=ALU.add
+                out=kern[g][:].rearrange("p i t j -> p t i j"),
+                in0=ramp[:].rearrange("p t (i j) -> p t i j", j=SIDE),
+                in1=tail[:].rearrange("p t (i j) -> p t i j", j=SIDE),
+                op=ALU.add,
             )
-            kern_t = keep.tile([P, 2, SIDE, SIDE], F32, name="kern_t%d" % pair)
-            for t in range(2):
-                nc.gpsimd.tensor_tensor(
-                    out=kern_t[:, t, :, :],
-                    in0=ramp[:, t, :].rearrange("p (i j) -> p j i", j=SIDE),
-                    in1=tail[:, t, :].rearrange("p (i j) -> p j i", j=SIDE),
-                    op=ALU.add,
-                )
-            kernels.append(kern)
-            kernels_t.append(kern_t)
+            kern_t.append(keep.tile([P, SIDE, GROUP_TILES, SIDE], F32, name="kern_t%d" % g))
+            nc.vector.tensor_copy(out=kern_t[g][:], in_=kern[g][:].rearrange("p i t j -> p j t i"))
 
         row = []
         col = []
         scaled = []
-        for pair in range(PAIRS):
-            row.append(keep.tile([P, 2, SIDE], F32, name="row%d" % pair))
-            col.append(keep.tile([P, 2, SIDE], F32, name="col%d" % pair))
-            scaled.append(keep.tile([P, 2, SIDE, SIDE], F32, name="scaled%d" % pair))
-            nc.vector.memset(row[pair][:], 1.0)
-            nc.vector.memset(col[pair][:], 1.0)
+        for g in range(GROUPS):
+            row.append(keep.tile([P, GROUP_TILES, SIDE], F32, name="row%d" % g))
+            col.append(keep.tile([P, GROUP_TILES, SIDE], F32, name="col%d" % g))
+            scaled.append(keep.tile([P, SIDE, GROUP_TILES, SIDE], F32, name="scaled%d" % g))
+            nc.vector.memset(row[g][:], 1.0)
+            nc.vector.memset(col[g][:], 1.0)
         for it in range(ROUNDS):
-            for pair in range(PAIRS):
+            for g in range(GROUPS):
                 if it == 0:
-                    update_factor(nc, small, col[pair], kernels[pair][:])
+                    update_factor(nc, psum_s, small, ident, col[g], kern[g])
                 else:
-                    scale_rows(nc, scaled[pair], kernels[pair], row[pair])
-                    update_factor(nc, small, col[pair], scaled[pair][:])
-            for pair in range(PAIRS):
-                scale_rows(nc, scaled[pair], kernels_t[pair], col[pair])
-                update_factor(nc, small, row[pair], scaled[pair][:])
-        for pair in range(PAIRS):
-            result = kernels[pair]
-            scale_rows(nc, result, scaled[pair][:].rearrange("p t j i -> p t i j"), row[pair])
-            for t in range(2):
-                m = 2 * pair + t
+                    scale_rows(nc, scaled[g], kern[g], row[g])
+                    update_factor(nc, psum_s, small, ident, col[g], scaled[g])
+            for g in range(GROUPS):
+                scale_rows(nc, scaled[g], kern_t[g], col[g])
+                update_factor(nc, psum_s, small, ident, row[g], scaled[g])
+        for g in range(GROUPS):
+            scale_rows(nc, scaled[g], kern[g], row[g])
+            result = keep.tile([P, GROUP_TILES, SIDE, SIDE], F32, name="result%d" % g)
+            nc.vector.tensor_tensor(
+                out=result[:].rearrange("p t i j -> p i t j"),
+                in0=scaled[g][:],
+                in1=col[g][:].unsqueeze(1).to_broadcast([P, SIDE, GROUP_TILES, SIDE]),
+                op=ALU.mult,
+            )
+            for t in range(GROUP_TILES):
+                m = GROUP_TILES * g + t
                 nc.sync.dma_start(
                     out=out[m * P : (m + 1) * P, :, :].rearrange("b i j -> b (i j)"),
                     in_=result[:, t, :, :].rearrange("p i j -> p (i j)"),

@@ -21,9 +21,9 @@ HID = 2048
 PASSES = HID // K_PASS
 TOKENS = 512
 TOKEN_TILES = TOKENS // P
-GROUPS = 2
+GROUPS = 4
 GROUP_TILES = TOKEN_TILES // GROUPS
-PIECES = 4
+PIECES = 2
 SIDE = 32
 DOUT = SIDE * SIDE
 N_TILE = 512
@@ -50,31 +50,28 @@ def load_weight_columns(nc, codes, words, cols):
     nc.sync.dma_start(out=codes[:, :, cols], in_=by_partition[:, :, cols])
 
 
-def quantise_rows(nc, psum_t, work, ident, rows, codes, planes):
-    words = rows.bitcast(F32)
-    grouped = work.tile([P, PASSES, P, PACK], BF16, tag="grouped", align_bytes=64)
-    for g in range(PASSES):
-        flipped = psum_t.tile([P, 2, P], F32, tag="flipped")
-        for u in range(2):
-            nc.tensor.transpose(flipped[:, u, :], words[:, 256 * g + u : 256 * (g + 1) : 2], ident[:])
-        nc.scalar.copy(
-            out=grouped[:, g, :, :].rearrange("p r (u e) -> p r u e", e=2),
-            in_=flipped[:].bitcast(BF16).rearrange("p u (r e) -> p r u e", e=2),
-        )
+def flip_pass(nc, psum_t, ident, words, g, grouped):
+    flipped = psum_t.tile([P, 2, P], F32, tag="flipped")
+    for u in range(2):
+        nc.tensor.transpose(flipped[:, u, :], words[:, 256 * g + u : 256 * (g + 1) : 2], ident[:])
+    nc.scalar.copy(
+        out=grouped.rearrange("p r (u e) -> p r u e", e=2),
+        in_=flipped[:].bitcast(BF16).rearrange("p u (r e) -> p r u e", e=2),
+    )
+
+
+def quantise(nc, grouped, codes, planes):
     nc.vector.quantize_mx(
-        out=codes.bitcast(FP8X4),
-        scales=planes,
-        in_=grouped[:].rearrange("p g r t -> p (g r t)"),
+        out=codes.bitcast(FP8X4), scales=planes, in_=grouped[:].rearrange("p a r t -> p (a r t)")
     )
 
 
 def mx_product(nc, acc, x_codes, x_planes, w_codes, w_planes, cols):
     for g in range(PASSES):
-        tokens = slice(g * P, (g + 1) * P)
         nc.tensor.matmul_mx(
             out=acc,
-            lhsT=x_codes[:, tokens].bitcast(FP8X4),
-            lhsT_scale=x_planes[:, tokens],
+            lhsT=x_codes[g].bitcast(FP8X4),
+            lhsT_scale=x_planes[g],
             rhs=w_codes[:, g, cols].bitcast(FP8X4),
             rhs_scale=w_planes[4 * g : P, cols],
             start=(g == 0),
@@ -94,9 +91,9 @@ def scale_rows(nc, scaled, mat, factor):
         )
 
 
-def update_factor(nc, psum_s, small, ident, factor, scaled):
+def update_factor(nc, psum_s, small, ident, fold, factor, scaled):
     blocks = SIDE // BLOCK_ROWS
-    across = psum_s.tile([P, P], F32, tag="across")
+    across = psum_s.tile([P, P], F32, tag="across", bufs=2)
     for b in range(blocks):
         nc.tensor.matmul(
             out=across[:],
@@ -109,15 +106,9 @@ def update_factor(nc, psum_s, small, ident, factor, scaled):
     across_sb = small.tile([P, P], F32, tag="across_sb")
     nc.scalar.copy(out=across_sb[:], in_=across[:])
     back = psum_s.tile([P, P], F32, tag="back")
-    nc.tensor.transpose(back[:], across_sb[:], ident[:])
+    nc.tensor.matmul(out=back[:], lhsT=across_sb[:], rhs=fold, start=True, stop=True)
     sums = small.tile([P, GROUP_TILES, SIDE], F32, tag="sums")
-    nc.vector.tensor_reduce(
-        out=sums[:].rearrange("p t y -> p (t y)"),
-        in_=back[:].rearrange("p (x c) -> p c x", x=BLOCK_ROWS),
-        axis=AXIS.X,
-        op=ALU.add,
-    )
-    nc.vector.reciprocal(out=sums[:], in_=sums[:])
+    nc.vector.reciprocal(out=sums[:].rearrange("p t y -> p (t y)"), in_=back[:, 0 : GROUP_TILES * SIDE])
     nc.vector.scalar_tensor_tensor(
         out=factor[:], in0=factor[:], scalar=1.0 / EPS, in1=sums[:], op0=ALU.mult, op1=ALU.min
     )
@@ -128,9 +119,9 @@ def tile_matchingnet_pa_kernel(tc, h3, W4_words, W4_scales, b4, W5_words, W5_sca
     with ExitStack() as stack:
         keep = stack.enter_context(tc.tile_pool(name="keep", bufs=1))
         work = stack.enter_context(tc.tile_pool(name="work", bufs=2))
-        small = stack.enter_context(tc.tile_pool(name="small", bufs=2))
+        small = stack.enter_context(tc.tile_pool(name="small", bufs=4))
         psum_t = stack.enter_context(tc.psum_pool(name="psum_t", bufs=2))
-        psum_acc = stack.enter_context(tc.psum_pool(name="psum_acc", bufs=4))
+        psum_acc = stack.enter_context(tc.psum_pool(name="psum_acc", bufs=3))
         psum_s = stack.enter_context(tc.psum_pool(name="psum_s", bufs=1))
 
         w4_codes, w4_planes = load_weight(nc, keep, W4_words, W4_scales, HID, "w4")
@@ -149,61 +140,105 @@ def tile_matchingnet_pa_kernel(tc, h3, W4_words, W4_scales, b4, W5_words, W5_sca
 
         ident = keep.tile([P, P], F32, name="ident")
         make_identity(nc, ident[:])
+        fold = keep.tile([P, BLOCK_ROWS, GROUP_TILES * SIDE], F32, name="fold")
+        nc.vector.tensor_reduce(
+            out=fold[:, 0, :], in_=ident[:].rearrange("p (x c) -> p c x", x=BLOCK_ROWS), axis=AXIS.X, op=ALU.add
+        )
+        nc.vector.tensor_copy(
+            out=fold[:, 1:, :],
+            in_=fold[:, 0:1, :].to_broadcast([P, BLOCK_ROWS - 1, GROUP_TILES * SIDE]),
+        )
         one = keep.tile([P, 1], F32, name="one")
         nc.vector.memset(one[:], 1.0)
 
-        x_codes = keep.tile([P, TOKEN_TILES, PASSES * P], I32, name="x_codes", align_bytes=64)
-        x_planes = keep.tile([P, TOKEN_TILES, PASSES * P], U8, name="x_planes", align_bytes=64)
-        h_codes = keep.tile([P, TOKEN_TILES, PASSES * P], I32, name="h_codes", align_bytes=64)
-        h_planes = keep.tile([P, TOKEN_TILES, PASSES * P], U8, name="h_planes", align_bytes=64)
+        x_codes = keep.tile([P, TOKEN_TILES, PASSES, P], I32, name="x_codes", align_bytes=64)
+        x_planes = keep.tile([P, TOKEN_TILES, PASSES, P], U8, name="x_planes", align_bytes=64)
+        h_codes = keep.tile([P, PASSES, TOKEN_TILES, P], I32, name="h_codes", align_bytes=64)
+        h_planes = keep.tile([P, PASSES, TOKEN_TILES, P], U8, name="h_planes", align_bytes=64)
+        h4 = keep.tile([P, TOKEN_TILES, HID], BF16, name="h4")
+
         for m in range(TOKEN_TILES):
-            quantise_rows(nc, psum_t, work, ident, x_rows[:, m, :], x_codes[:, m, :], x_planes[:, m, :])
+            grouped = work.tile([P, PASSES, P, PACK], BF16, tag="grouped", align_bytes=64)
+            for g in range(PASSES):
+                flip_pass(nc, psum_t, ident, x_rows[:, m, :].bitcast(F32), g, grouped[:, g, :, :])
+            quantise(
+                nc,
+                grouped,
+                x_codes[:, m, :, :].rearrange("p g r -> p (g r)"),
+                x_planes[:, m, :, :].rearrange("p g r -> p (g r)"),
+            )
 
-        def layer_1(m):
-            h4 = work.tile([P, HID], BF16, tag="h4")
-            for c in range(HID // N_TILE):
-                cols = slice(c * N_TILE, (c + 1) * N_TILE)
-                acc = psum_acc.tile([P, N_TILE], F32, tag="acc")
-                mx_product(nc, acc[:], x_codes[:, m, :], x_planes[:, m, :], w4_codes, w4_planes, cols)
-                pre = work.tile([P, N_TILE], F32, tag="pre", bufs=3)
-                nc.vector.tensor_tensor(out=pre[:], in0=acc[:], in1=b4_all[:, cols], op=ALU.add)
-                low = work.tile([P, N_TILE], F32, tag="low", bufs=3)
-                nc.scalar.activation(out=low[:], in_=pre[:], func=ACT.Copy, scale=SLOPE)
-                nc.vector.tensor_tensor(out=h4[:, cols], in0=pre[:], in1=low[:], op=ALU.max)
-            return h4
+        def layer_1(m, c):
+            cols = slice(c * N_TILE, (c + 1) * N_TILE)
+            acc = psum_acc.tile([P, N_TILE], F32, tag="acc")
+            mx_product(
+                nc,
+                acc[:],
+                [x_codes[:, m, g, :] for g in range(PASSES)],
+                [x_planes[:, m, g, :] for g in range(PASSES)],
+                w4_codes,
+                w4_planes,
+                cols,
+            )
+            pre = work.tile([P, N_TILE], F32, tag="pre", bufs=3)
+            nc.vector.tensor_tensor(out=pre[:], in0=acc[:], in1=b4_all[:, cols], op=ALU.add)
+            low = work.tile([P, N_TILE], F32, tag="low", bufs=3)
+            nc.gpsimd.tensor_scalar(out=low[:], in0=pre[:], scalar1=SLOPE, scalar2=0.0, op0=ALU.mult, op1=ALU.add)
+            nc.vector.tensor_tensor(out=h4[:, m, cols], in0=pre[:], in1=low[:], op=ALU.max)
 
-        def layer_2(m, h4, z):
-            quantise_rows(nc, psum_t, work, ident, h4[:], h_codes[:, m, :], h_planes[:, m, :])
+        def quantise_h4(g):
+            grouped = work.tile([P, TOKEN_TILES, P, PACK], BF16, tag="grouped", align_bytes=64)
+            for m in range(TOKEN_TILES):
+                flip_pass(nc, psum_t, ident, h4[:, m, :].bitcast(F32), g, grouped[:, m, :, :])
+            quantise(
+                nc,
+                grouped,
+                h_codes[:, g, :, :].rearrange("p m r -> p (m r)"),
+                h_planes[:, g, :, :].rearrange("p m r -> p (m r)"),
+            )
+
+        for c in range(PASSES):
+            for m in range(TOKEN_TILES):
+                layer_1(m, c)
+            if c > 0:
+                quantise_h4(c - 1)
+        quantise_h4(PASSES - 1)
+
+        z = keep.tile([P, TOKEN_TILES, DOUT], F32, name="z")
+        tail = keep.tile([P, TOKEN_TILES, DOUT], F32, name="tail")
+        for m in range(TOKEN_TILES):
             for c in range(DOUT // N_TILE):
                 cols = slice(c * N_TILE, (c + 1) * N_TILE)
                 acc = psum_acc.tile([P, N_TILE], F32, tag="acc")
-                mx_product(nc, acc[:], h_codes[:, m, :], h_planes[:, m, :], w5_codes, w5_planes, cols)
-                nc.vector.tensor_tensor(out=z[:, cols], in0=acc[:], in1=b5_all[:, cols], op=ALU.add)
-
+                mx_product(
+                    nc,
+                    acc[:],
+                    [h_codes[:, k, m, :] for k in range(PASSES)],
+                    [h_planes[:, k, m, :] for k in range(PASSES)],
+                    w5_codes,
+                    w5_planes,
+                    cols,
+                )
+                nc.vector.tensor_tensor(out=z[:, m, cols], in0=acc[:], in1=b5_all[:, cols], op=ALU.add)
+            nc.scalar.activation(out=tail[:, m, :], in_=z[:, m, :], func=ACT.Abs)
+            nc.scalar.activation(out=tail[:, m, :], in_=tail[:, m, :], func=ACT.Exp, scale=-1.0)
+            nc.gpsimd.tensor_scalar(out=z[:, m, :], in0=z[:, m, :], scalar1=0.0, scalar2=0.0, op0=ALU.max, op1=ALU.add)
         kern = []
         kern_t = []
         for g in range(GROUPS):
-            z = work.tile([P, GROUP_TILES, DOUT], F32, tag="z", bufs=1)
-            first = layer_1(GROUP_TILES * g)
-            second = layer_1(GROUP_TILES * g + 1)
-            layer_2(GROUP_TILES * g, first, z[:, 0, :])
-            layer_2(GROUP_TILES * g + 1, second, z[:, 1, :])
-
-            tail = work.tile([P, GROUP_TILES, DOUT], F32, tag="tail", bufs=1)
-            nc.scalar.activation(out=tail[:], in_=z[:], func=ACT.Abs)
-            nc.scalar.activation(out=tail[:], in_=tail[:], func=ACT.Exp, scale=-1.0)
-            nc.scalar.activation(out=tail[:], in_=tail[:], func=ACT.Ln, bias=one[:])
-            ramp = work.tile([P, GROUP_TILES, DOUT], F32, tag="ramp", bufs=1)
-            nc.scalar.activation(out=ramp[:], in_=z[:], func=ACT.Relu)
             kern.append(keep.tile([P, SIDE, GROUP_TILES, SIDE], F32, name="kern%d" % g))
-            nc.gpsimd.tensor_tensor(
-                out=kern[g][:].rearrange("p i t j -> p t i j"),
-                in0=ramp[:].rearrange("p t (i j) -> p t i j", j=SIDE),
-                in1=tail[:].rearrange("p t (i j) -> p t i j", j=SIDE),
-                op=ALU.add,
-            )
             kern_t.append(keep.tile([P, SIDE, GROUP_TILES, SIDE], F32, name="kern_t%d" % g))
-            nc.vector.tensor_copy(out=kern_t[g][:], in_=kern[g][:].rearrange("p i t j -> p j t i"))
+            for t in range(GROUP_TILES):
+                m = GROUP_TILES * g + t
+                nc.scalar.activation(out=tail[:, m, :], in_=tail[:, m, :], func=ACT.Ln, bias=one[:])
+                nc.vector.tensor_tensor(
+                    out=kern[g][:, :, t, :],
+                    in0=z[:, m, :].rearrange("p (i j) -> p i j", j=SIDE),
+                    in1=tail[:, m, :].rearrange("p (i j) -> p i j", j=SIDE),
+                    op=ALU.add,
+                )
+        for g in range(GROUPS):
+            nc.scalar.copy(out=kern_t[g][:], in_=kern[g][:].rearrange("p i t j -> p j t i"))
 
         row = []
         col = []
@@ -217,18 +252,18 @@ def tile_matchingnet_pa_kernel(tc, h3, W4_words, W4_scales, b4, W5_words, W5_sca
         for it in range(ROUNDS):
             for g in range(GROUPS):
                 if it == 0:
-                    update_factor(nc, psum_s, small, ident, col[g], kern[g])
+                    update_factor(nc, psum_s, small, ident, fold[:].rearrange("p x c -> p (x c)"), col[g], kern[g])
                 else:
                     scale_rows(nc, scaled[g], kern[g], row[g])
-                    update_factor(nc, psum_s, small, ident, col[g], scaled[g])
+                    update_factor(nc, psum_s, small, ident, fold[:].rearrange("p x c -> p (x c)"), col[g], scaled[g])
             for g in range(GROUPS):
                 scale_rows(nc, scaled[g], kern_t[g], col[g])
-                update_factor(nc, psum_s, small, ident, row[g], scaled[g])
+                update_factor(nc, psum_s, small, ident, fold[:].rearrange("p x c -> p (x c)"), row[g], scaled[g])
         for g in range(GROUPS):
             scale_rows(nc, scaled[g], kern[g], row[g])
-            result = keep.tile([P, GROUP_TILES, SIDE, SIDE], F32, name="result%d" % g)
+            result = z[:, GROUP_TILES * g : GROUP_TILES * (g + 1), :].rearrange("p t (i j) -> p t i j", j=SIDE)
             nc.vector.tensor_tensor(
-                out=result[:].rearrange("p t i j -> p i t j"),
+                out=result.rearrange("p t i j -> p i t j"),
                 in0=scaled[g][:],
                 in1=col[g][:].unsqueeze(1).to_broadcast([P, SIDE, GROUP_TILES, SIDE]),
                 op=ALU.mult,

@@ -30,6 +30,7 @@ N_TILE = 512
 SLOPE = 0.01
 EPS = 1e-8
 ROUNDS = 10
+PIECE_ROWS = SIDE // PIECES
 BLOCK_ROWS = P // (GROUP_TILES * SIDE)
 
 
@@ -79,39 +80,27 @@ def mx_product(nc, acc, x_codes, x_planes, w_codes, w_planes, cols):
         )
 
 
-def scale_rows(nc, scaled, mat, factor):
-    step = SIDE // PIECES
-    for piece in range(PIECES):
-        rows = slice(piece * step, (piece + 1) * step)
-        nc.vector.tensor_tensor(
-            out=scaled[:, rows, :, :],
-            in0=mat[:, rows, :, :],
-            in1=factor[:, :, rows].rearrange("p t x -> p x t").unsqueeze(3).to_broadcast([P, step, GROUP_TILES, SIDE]),
-            op=ALU.mult,
-        )
+def scale_piece(nc, scaled, mat, factor, piece):
+    rows = slice(piece * PIECE_ROWS, (piece + 1) * PIECE_ROWS)
+    nc.vector.tensor_tensor(
+        out=scaled[:, rows, :, :],
+        in0=mat[:, rows, :, :],
+        in1=factor[:, :, rows].rearrange("p t x -> p x t").unsqueeze(3).to_broadcast([P, PIECE_ROWS, GROUP_TILES, SIDE]),
+        op=ALU.mult,
+    )
 
 
-def update_factor(nc, psum_s, small, ident, fold, factor, scaled):
-    blocks = SIDE // BLOCK_ROWS
-    across = psum_s.tile([P, P], F32, tag="across", bufs=2)
-    for b in range(blocks):
+def add_up_piece(nc, across, ident, scaled, piece):
+    blocks = PIECE_ROWS // BLOCK_ROWS
+    for b in range(piece * blocks, (piece + 1) * blocks):
         nc.tensor.matmul(
             out=across[:],
             lhsT=scaled[:, b * BLOCK_ROWS : (b + 1) * BLOCK_ROWS, :, :].rearrange("p x t y -> p (x t y)"),
             rhs=ident[:],
             is_transpose=True,
             start=(b == 0),
-            stop=(b == blocks - 1),
+            stop=(b == SIDE // BLOCK_ROWS - 1),
         )
-    across_sb = small.tile([P, P], F32, tag="across_sb")
-    nc.scalar.copy(out=across_sb[:], in_=across[:])
-    back = psum_s.tile([P, P], F32, tag="back")
-    nc.tensor.matmul(out=back[:], lhsT=across_sb[:], rhs=fold, start=True, stop=True)
-    sums = small.tile([P, GROUP_TILES, SIDE], F32, tag="sums")
-    nc.vector.reciprocal(out=sums[:].rearrange("p t y -> p (t y)"), in_=back[:, 0 : GROUP_TILES * SIDE])
-    nc.vector.scalar_tensor_tensor(
-        out=factor[:], in0=factor[:], scalar=1.0 / EPS, in1=sums[:], op0=ALU.mult, op1=ALU.min
-    )
 
 
 def tile_matchingnet_pa_kernel(tc, h3, W4_words, W4_scales, b4, W5_words, W5_scales, b5, out):
@@ -120,9 +109,6 @@ def tile_matchingnet_pa_kernel(tc, h3, W4_words, W4_scales, b4, W5_words, W5_sca
         keep = stack.enter_context(tc.tile_pool(name="keep", bufs=1))
         work = stack.enter_context(tc.tile_pool(name="work", bufs=2))
         small = stack.enter_context(tc.tile_pool(name="small", bufs=4))
-        psum_t = stack.enter_context(tc.psum_pool(name="psum_t", bufs=2))
-        psum_acc = stack.enter_context(tc.psum_pool(name="psum_acc", bufs=3))
-        psum_s = stack.enter_context(tc.psum_pool(name="psum_s", bufs=1))
 
         w4_codes, w4_planes = load_weight(nc, keep, W4_words, W4_scales, HID, "w4")
         w5_codes, w5_planes = load_weight(nc, keep, W5_words, W5_scales, DOUT, "w5")
@@ -140,106 +126,102 @@ def tile_matchingnet_pa_kernel(tc, h3, W4_words, W4_scales, b4, W5_words, W5_sca
 
         ident = keep.tile([P, P], F32, name="ident")
         make_identity(nc, ident[:])
-        fold = keep.tile([P, BLOCK_ROWS, GROUP_TILES * SIDE], F32, name="fold")
+        fold = keep.tile([P, GROUP_TILES * SIDE], F32, name="fold")
         nc.vector.tensor_reduce(
-            out=fold[:, 0, :], in_=ident[:].rearrange("p (x c) -> p c x", x=BLOCK_ROWS), axis=AXIS.X, op=ALU.add
-        )
-        nc.vector.tensor_copy(
-            out=fold[:, 1:, :],
-            in_=fold[:, 0:1, :].to_broadcast([P, BLOCK_ROWS - 1, GROUP_TILES * SIDE]),
+            out=fold[:], in_=ident[:].rearrange("p (x c) -> p c x", x=BLOCK_ROWS), axis=AXIS.X, op=ALU.add
         )
         one = keep.tile([P, 1], F32, name="one")
         nc.vector.memset(one[:], 1.0)
 
-        x_codes = keep.tile([P, TOKEN_TILES, PASSES, P], I32, name="x_codes", align_bytes=64)
-        x_planes = keep.tile([P, TOKEN_TILES, PASSES, P], U8, name="x_planes", align_bytes=64)
-        h_codes = keep.tile([P, PASSES, TOKEN_TILES, P], I32, name="h_codes", align_bytes=64)
-        h_planes = keep.tile([P, PASSES, TOKEN_TILES, P], U8, name="h_planes", align_bytes=64)
-        h4 = keep.tile([P, TOKEN_TILES, HID], BF16, name="h4")
+        with tc.psum_pool(name="psum_t", bufs=2) as psum_t, tc.psum_pool(name="psum_acc", bufs=6) as psum_acc:
+            x_codes = keep.tile([P, TOKEN_TILES, PASSES, P], I32, name="x_codes", align_bytes=64)
+            x_planes = keep.tile([P, TOKEN_TILES, PASSES, P], U8, name="x_planes", align_bytes=64)
+            h_codes = keep.tile([P, PASSES, TOKEN_TILES, P], I32, name="h_codes", align_bytes=64)
+            h_planes = keep.tile([P, PASSES, TOKEN_TILES, P], U8, name="h_planes", align_bytes=64)
+            h4 = keep.tile([P, TOKEN_TILES, HID], BF16, name="h4")
 
-        for m in range(TOKEN_TILES):
-            grouped = work.tile([P, PASSES, P, PACK], BF16, tag="grouped", align_bytes=64)
-            for g in range(PASSES):
-                flip_pass(nc, psum_t, ident, x_rows[:, m, :].bitcast(F32), g, grouped[:, g, :, :])
-            quantise(
-                nc,
-                grouped,
-                x_codes[:, m, :, :].rearrange("p g r -> p (g r)"),
-                x_planes[:, m, :, :].rearrange("p g r -> p (g r)"),
-            )
-
-        def layer_1(m, c):
-            cols = slice(c * N_TILE, (c + 1) * N_TILE)
-            acc = psum_acc.tile([P, N_TILE], F32, tag="acc")
-            mx_product(
-                nc,
-                acc[:],
-                [x_codes[:, m, g, :] for g in range(PASSES)],
-                [x_planes[:, m, g, :] for g in range(PASSES)],
-                w4_codes,
-                w4_planes,
-                cols,
-            )
-            pre = work.tile([P, N_TILE], F32, tag="pre", bufs=3)
-            nc.vector.tensor_tensor(out=pre[:], in0=acc[:], in1=b4_all[:, cols], op=ALU.add)
-            low = work.tile([P, N_TILE], F32, tag="low", bufs=3)
-            nc.gpsimd.tensor_scalar(out=low[:], in0=pre[:], scalar1=SLOPE, scalar2=0.0, op0=ALU.mult, op1=ALU.add)
-            nc.vector.tensor_tensor(out=h4[:, m, cols], in0=pre[:], in1=low[:], op=ALU.max)
-
-        def quantise_h4(g):
-            grouped = work.tile([P, TOKEN_TILES, P, PACK], BF16, tag="grouped", align_bytes=64)
             for m in range(TOKEN_TILES):
-                flip_pass(nc, psum_t, ident, h4[:, m, :].bitcast(F32), g, grouped[:, m, :, :])
-            quantise(
-                nc,
-                grouped,
-                h_codes[:, g, :, :].rearrange("p m r -> p (m r)"),
-                h_planes[:, g, :, :].rearrange("p m r -> p (m r)"),
-            )
+                grouped = work.tile([P, PASSES, P, PACK], BF16, tag="grouped", align_bytes=64)
+                for g in range(PASSES):
+                    flip_pass(nc, psum_t, ident, x_rows[:, m, :].bitcast(F32), g, grouped[:, g, :, :])
+                quantise(
+                    nc,
+                    grouped,
+                    x_codes[:, m, :, :].rearrange("p g r -> p (g r)"),
+                    x_planes[:, m, :, :].rearrange("p g r -> p (g r)"),
+                )
 
-        for c in range(PASSES):
-            for m in range(TOKEN_TILES):
-                layer_1(m, c)
-            if c > 0:
-                quantise_h4(c - 1)
-        quantise_h4(PASSES - 1)
-
-        z = keep.tile([P, TOKEN_TILES, DOUT], F32, name="z")
-        tail = keep.tile([P, TOKEN_TILES, DOUT], F32, name="tail")
-        for m in range(TOKEN_TILES):
-            for c in range(DOUT // N_TILE):
+            def layer_1(m, c):
                 cols = slice(c * N_TILE, (c + 1) * N_TILE)
                 acc = psum_acc.tile([P, N_TILE], F32, tag="acc")
                 mx_product(
                     nc,
                     acc[:],
-                    [h_codes[:, k, m, :] for k in range(PASSES)],
-                    [h_planes[:, k, m, :] for k in range(PASSES)],
-                    w5_codes,
-                    w5_planes,
+                    [x_codes[:, m, g, :] for g in range(PASSES)],
+                    [x_planes[:, m, g, :] for g in range(PASSES)],
+                    w4_codes,
+                    w4_planes,
                     cols,
                 )
-                nc.vector.tensor_tensor(out=z[:, m, cols], in0=acc[:], in1=b5_all[:, cols], op=ALU.add)
-            nc.scalar.activation(out=tail[:, m, :], in_=z[:, m, :], func=ACT.Abs)
-            nc.scalar.activation(out=tail[:, m, :], in_=tail[:, m, :], func=ACT.Exp, scale=-1.0)
-            nc.gpsimd.tensor_scalar(out=z[:, m, :], in0=z[:, m, :], scalar1=0.0, scalar2=0.0, op0=ALU.max, op1=ALU.add)
-        kern = []
-        kern_t = []
-        for g in range(GROUPS):
-            kern.append(keep.tile([P, SIDE, GROUP_TILES, SIDE], F32, name="kern%d" % g))
-            kern_t.append(keep.tile([P, SIDE, GROUP_TILES, SIDE], F32, name="kern_t%d" % g))
-            for t in range(GROUP_TILES):
-                m = GROUP_TILES * g + t
-                nc.scalar.activation(out=tail[:, m, :], in_=tail[:, m, :], func=ACT.Ln, bias=one[:])
-                nc.vector.tensor_tensor(
-                    out=kern[g][:, :, t, :],
-                    in0=z[:, m, :].rearrange("p (i j) -> p i j", j=SIDE),
-                    in1=tail[:, m, :].rearrange("p (i j) -> p i j", j=SIDE),
-                    op=ALU.add,
-                )
-        for g in range(GROUPS):
-            nc.scalar.copy(out=kern_t[g][:], in_=kern[g][:].rearrange("p i t j -> p j t i"))
+                pre = work.tile([P, N_TILE], F32, tag="pre", bufs=3)
+                nc.vector.tensor_tensor(out=pre[:], in0=acc[:], in1=b4_all[:, cols], op=ALU.add)
+                low = work.tile([P, N_TILE], F32, tag="low", bufs=3)
+                nc.gpsimd.tensor_scalar(out=low[:], in0=pre[:], scalar1=SLOPE, scalar2=0.0, op0=ALU.mult, op1=ALU.add)
+                nc.vector.tensor_tensor(out=h4[:, m, cols], in0=pre[:], in1=low[:], op=ALU.max)
 
+            def quantise_h4(g):
+                grouped = work.tile([P, TOKEN_TILES, P, PACK], BF16, tag="grouped", align_bytes=64)
+                for m in range(TOKEN_TILES):
+                    flip_pass(nc, psum_t, ident, h4[:, m, :].bitcast(F32), g, grouped[:, m, :, :])
+                quantise(
+                    nc,
+                    grouped,
+                    h_codes[:, g, :, :].rearrange("p m r -> p (m r)"),
+                    h_planes[:, g, :, :].rearrange("p m r -> p (m r)"),
+                )
+
+            for c in range(PASSES):
+                for m in range(TOKEN_TILES):
+                    layer_1(m, c)
+                if c > 0:
+                    quantise_h4(c - 1)
+            quantise_h4(PASSES - 1)
+
+            z = keep.tile([P, TOKEN_TILES, DOUT], F32, name="z")
+            tail = keep.tile([P, TOKEN_TILES, DOUT], F32, name="tail")
+            for m in range(TOKEN_TILES):
+                for c in range(DOUT // N_TILE):
+                    cols = slice(c * N_TILE, (c + 1) * N_TILE)
+                    acc = psum_acc.tile([P, N_TILE], F32, tag="acc")
+                    mx_product(
+                        nc,
+                        acc[:],
+                        [h_codes[:, k, m, :] for k in range(PASSES)],
+                        [h_planes[:, k, m, :] for k in range(PASSES)],
+                        w5_codes,
+                        w5_planes,
+                        cols,
+                    )
+                    nc.vector.tensor_tensor(out=z[:, m, cols], in0=acc[:], in1=b5_all[:, cols], op=ALU.add)
+                nc.scalar.activation(out=tail[:, m, :], in_=z[:, m, :], func=ACT.Abs)
+                nc.scalar.activation(out=tail[:, m, :], in_=tail[:, m, :], func=ACT.Exp, scale=-1.0)
+                nc.gpsimd.tensor_scalar(out=z[:, m, :], in0=z[:, m, :], scalar1=0.0, scalar2=0.0, op0=ALU.max, op1=ALU.add)
+            kern = []
+            kern_t = []
+            for g in range(GROUPS):
+                kern.append(keep.tile([P, SIDE, GROUP_TILES, SIDE], F32, name="kern%d" % g))
+                kern_t.append(keep.tile([P, SIDE, GROUP_TILES, SIDE], F32, name="kern_t%d" % g))
+                for t in range(GROUP_TILES):
+                    m = GROUP_TILES * g + t
+                    nc.scalar.activation(out=tail[:, m, :], in_=tail[:, m, :], func=ACT.Ln, bias=one[:])
+                    nc.vector.tensor_tensor(
+                        out=kern[g][:, :, t, :],
+                        in0=z[:, m, :].rearrange("p (i j) -> p i j", j=SIDE),
+                        in1=tail[:, m, :].rearrange("p (i j) -> p i j", j=SIDE),
+                        op=ALU.add,
+                    )
+
+        psum_s = stack.enter_context(tc.psum_pool(name="psum_s", bufs=3))
         row = []
         col = []
         scaled = []
@@ -249,28 +231,58 @@ def tile_matchingnet_pa_kernel(tc, h3, W4_words, W4_scales, b4, W5_words, W5_sca
             scaled.append(keep.tile([P, SIDE, GROUP_TILES, SIDE], F32, name="scaled%d" % g))
             nc.vector.memset(row[g][:], 1.0)
             nc.vector.memset(col[g][:], 1.0)
+
+        steps = []
         for it in range(ROUNDS):
+            steps.extend((g, kern[g], row[g], col[g]) for g in range(GROUPS))
+            steps.extend((g, kern_t[g], col[g], row[g]) for g in range(GROUPS))
+
+        across = {}
+        back = {}
+        with tc.manual_schedule():
+            for n in range(len(steps) + 3):
+                if 0 <= n - 1 < len(steps):
+                    across_sb = small.tile([P, P], F32, tag="across_sb")
+                    nc.scalar.copy(out=across_sb[:], in_=across[n - 1][:])
+                for piece in range(PIECES):
+                    if piece == 0 and 0 <= n - 3:
+                        inverse = small.tile([P, GROUP_TILES, SIDE], F32, tag="inverse")
+                        nc.vector.reciprocal(out=inverse[:].rearrange("p t y -> p (t y)"), in_=back[n - 3][:])
+                    if piece == 1 and 0 <= n - 3:
+                        renewed = steps[n - 3][3]
+                        nc.vector.scalar_tensor_tensor(
+                            out=renewed[:], in0=renewed[:], scalar=1.0 / EPS, in1=inverse[:], op0=ALU.mult, op1=ALU.min
+                        )
+                    if n < len(steps):
+                        g, mat, scale = steps[n][0:3]
+                        if piece == 0:
+                            across[n] = psum_s.tile([P, P], F32, name="across", tag="across")
+                        if n < GROUPS:
+                            add_up_piece(nc, across[n], ident, mat, piece)
+                            rows = slice(piece * PIECE_ROWS, (piece + 1) * PIECE_ROWS)
+                            nc.vector.tensor_copy(
+                                out=kern_t[g][:, rows, :, :], in_=mat[:, :, :, rows].rearrange("p i t j -> p j t i")
+                            )
+                        else:
+                            scale_piece(nc, scaled[g], mat, scale, piece)
+                            add_up_piece(nc, across[n], ident, scaled[g], piece)
+                if 0 <= n - 1 < len(steps):
+                    back[n - 1] = psum_s.tile([P, GROUP_TILES * SIDE], F32, name="back", tag="back")
+                    nc.tensor.matmul(out=back[n - 1][:], lhsT=across_sb[:], rhs=fold[:], start=True, stop=True)
+
             for g in range(GROUPS):
-                if it == 0:
-                    update_factor(nc, psum_s, small, ident, fold[:].rearrange("p x c -> p (x c)"), col[g], kern[g])
-                else:
-                    scale_rows(nc, scaled[g], kern[g], row[g])
-                    update_factor(nc, psum_s, small, ident, fold[:].rearrange("p x c -> p (x c)"), col[g], scaled[g])
-            for g in range(GROUPS):
-                scale_rows(nc, scaled[g], kern_t[g], col[g])
-                update_factor(nc, psum_s, small, ident, fold[:].rearrange("p x c -> p (x c)"), row[g], scaled[g])
-        for g in range(GROUPS):
-            scale_rows(nc, scaled[g], kern[g], row[g])
-            result = z[:, GROUP_TILES * g : GROUP_TILES * (g + 1), :].rearrange("p t (i j) -> p t i j", j=SIDE)
-            nc.vector.tensor_tensor(
-                out=result.rearrange("p t i j -> p i t j"),
-                in0=scaled[g][:],
-                in1=col[g][:].unsqueeze(1).to_broadcast([P, SIDE, GROUP_TILES, SIDE]),
-                op=ALU.mult,
-            )
-            for t in range(GROUP_TILES):
-                m = GROUP_TILES * g + t
-                nc.sync.dma_start(
-                    out=out[m * P : (m + 1) * P, :, :].rearrange("b i j -> b (i j)"),
-                    in_=result[:, t, :, :].rearrange("p i j -> p (i j)"),
+                for piece in range(PIECES):
+                    scale_piece(nc, scaled[g], kern[g], row[g], piece)
+                result = z[:, GROUP_TILES * g : GROUP_TILES * (g + 1), :].rearrange("p t (i j) -> p t i j", j=SIDE)
+                nc.vector.tensor_tensor(
+                    out=result.rearrange("p t i j -> p i t j"),
+                    in0=scaled[g][:],
+                    in1=col[g][:].unsqueeze(1).to_broadcast([P, SIDE, GROUP_TILES, SIDE]),
+                    op=ALU.mult,
                 )
+                for t in range(GROUP_TILES):
+                    m = GROUP_TILES * g + t
+                    nc.sync.dma_start(
+                        out=out[m * P : (m + 1) * P, :, :].rearrange("b i j -> b (i j)"),
+                        in_=result[:, t, :, :].rearrange("p i j -> p (i j)"),
+                    )

@@ -32,6 +32,7 @@ EPS = 1e-8
 ROUNDS = 10
 PIECE_ROWS = SIDE // PIECES
 BLOCK_ROWS = P // (GROUP_TILES * SIDE)
+FOLD_REPEAT = 6
 
 
 def load_weight(nc, keep, words, scales, n_cols, name):
@@ -126,9 +127,12 @@ def tile_matchingnet_pa_kernel(tc, h3, W4_words, W4_scales, b4, W5_words, W5_sca
 
         ident = keep.tile([P, P], F32, name="ident")
         make_identity(nc, ident[:])
-        fold = keep.tile([P, GROUP_TILES * SIDE], F32, name="fold")
+        fold = keep.tile([P, FOLD_REPEAT, GROUP_TILES * SIDE], F32, name="fold")
         nc.vector.tensor_reduce(
-            out=fold[:], in_=ident[:].rearrange("p (x c) -> p c x", x=BLOCK_ROWS), axis=AXIS.X, op=ALU.add
+            out=fold[:, 0, :], in_=ident[:].rearrange("p (x c) -> p c x", x=BLOCK_ROWS), axis=AXIS.X, op=ALU.add
+        )
+        nc.vector.tensor_copy(
+            out=fold[:, 1:, :], in_=fold[:, 0:1, :].to_broadcast([P, FOLD_REPEAT - 1, GROUP_TILES * SIDE])
         )
         one = keep.tile([P, 1], F32, name="one")
         nc.vector.memset(one[:], 1.0)
@@ -247,7 +251,7 @@ def tile_matchingnet_pa_kernel(tc, h3, W4_words, W4_scales, b4, W5_words, W5_sca
                 for piece in range(PIECES):
                     if piece == 0 and 0 <= n - 3:
                         inverse = small.tile([P, GROUP_TILES, SIDE], F32, tag="inverse")
-                        nc.vector.reciprocal(out=inverse[:].rearrange("p t y -> p (t y)"), in_=back[n - 3][:])
+                        nc.vector.reciprocal(out=inverse[:].rearrange("p t y -> p (t y)"), in_=back[n - 3][:, 0 : GROUP_TILES * SIDE])
                     if piece == 1 and 0 <= n - 3:
                         renewed = steps[n - 3][3]
                         nc.vector.scalar_tensor_tensor(
@@ -267,8 +271,10 @@ def tile_matchingnet_pa_kernel(tc, h3, W4_words, W4_scales, b4, W5_words, W5_sca
                             scale_piece(nc, scaled[g], mat, scale, piece)
                             add_up_piece(nc, across[n], ident, scaled[g], piece)
                 if 0 <= n - 1 < len(steps):
-                    back[n - 1] = psum_s.tile([P, GROUP_TILES * SIDE], F32, name="back", tag="back")
-                    nc.tensor.matmul(out=back[n - 1][:], lhsT=across_sb[:], rhs=fold[:], start=True, stop=True)
+                    back[n - 1] = psum_s.tile([P, FOLD_REPEAT * GROUP_TILES * SIDE], F32, name="back", tag="back")
+                    nc.tensor.matmul(
+                        out=back[n - 1][:], lhsT=across_sb[:], rhs=fold[:].rearrange("p r c -> p (r c)"), start=True, stop=True
+                    )
 
             for g in range(GROUPS):
                 for piece in range(PIECES):

@@ -19,35 +19,31 @@ PACK = 4
 K_PASS = P * PACK
 HID = 2048
 PASSES = HID // K_PASS
-TOKENS = 512
-TOKEN_TILES = TOKENS // P
-GROUPS = 4
-GROUP_TILES = TOKEN_TILES // GROUPS
-PIECES = 2
+TOKEN_TILES = 512 // P
 SIDE = 32
 DOUT = SIDE * SIDE
 N_TILE = 512
 SLOPE = 0.01
 EPS = 1e-8
 ROUNDS = 10
-PIECE_ROWS = SIDE // PIECES
-BLOCK_ROWS = P // (GROUP_TILES * SIDE)
+BLOCK_ROWS = P // SIDE
+HALF = SIDE // 2
+SCALAR_ROWS = BLOCK_ROWS
 FOLD_REPEAT = 6
 
 
-def load_weight(nc, keep, words, scales, n_cols, name):
-    planes = keep.tile([P, n_cols], U8, name=name + "_planes", align_bytes=64)
+def load_scale_planes(nc, keep, scales, n_cols, name):
+    planes = keep.tile([P, n_cols], U8, name=name, align_bytes=64)
     nc.vector.memset(planes[:].bitcast(I32), 0)
     for quadrant in range(4):
         nc.sync.dma_start(
             out=planes[32 * quadrant : 32 * quadrant + 16, :].bitcast(I32),
             in_=scales[:, 4 * quadrant : 4 * quadrant + 4, :].bitcast(I32),
         )
-    codes = keep.tile([P, PASSES, n_cols], I32, name=name + "_codes", align_bytes=64)
-    return codes, planes
+    return planes
 
 
-def load_weight_columns(nc, codes, words, cols):
+def load_words(nc, codes, words, cols):
     by_partition = words.rearrange("g p n t -> g p (n t)").bitcast(I32).rearrange("g p n -> p g n")
     nc.sync.dma_start(out=codes[:, :, cols], in_=by_partition[:, :, cols])
 
@@ -81,22 +77,25 @@ def mx_product(nc, acc, x_codes, x_planes, w_codes, w_planes, cols):
         )
 
 
-def scale_piece(nc, scaled, mat, factor, piece):
-    rows = slice(piece * PIECE_ROWS, (piece + 1) * PIECE_ROWS)
+def scale_rows(nc, scaled, mat, factor, first, last):
     nc.vector.tensor_tensor(
-        out=scaled[:, rows, :, :],
-        in0=mat[:, rows, :, :],
-        in1=factor[:, :, rows].rearrange("p t x -> p x t").unsqueeze(3).to_broadcast([P, PIECE_ROWS, GROUP_TILES, SIDE]),
+        out=scaled[:, first:last, :],
+        in0=mat[:, first:last, :],
+        in1=factor[:, first:last].unsqueeze(2).to_broadcast([P, last - first, SIDE]),
         op=ALU.mult,
     )
 
 
-def add_up_piece(nc, across, ident, scaled, piece):
-    blocks = PIECE_ROWS // BLOCK_ROWS
-    for b in range(piece * blocks, (piece + 1) * blocks):
+def scale_rows_on_scalar(nc, scaled, mat, factor, first, last):
+    for x in range(first, last):
+        nc.scalar.activation(out=scaled[:, x, :], in_=mat[:, x, :], func=ACT.Copy, scale=factor[:, x : x + 1])
+
+
+def add_up(nc, across, ident, scaled, first, last):
+    for b in range(first // BLOCK_ROWS, last // BLOCK_ROWS):
         nc.tensor.matmul(
             out=across[:],
-            lhsT=scaled[:, b * BLOCK_ROWS : (b + 1) * BLOCK_ROWS, :, :].rearrange("p x t y -> p (x t y)"),
+            lhsT=scaled[:, b * BLOCK_ROWS : (b + 1) * BLOCK_ROWS, :].rearrange("p x y -> p (x y)"),
             rhs=ident[:],
             is_transpose=True,
             start=(b == 0),
@@ -111,15 +110,17 @@ def tile_matchingnet_pa_kernel(tc, h3, W4_words, W4_scales, b4, W5_words, W5_sca
         work = stack.enter_context(tc.tile_pool(name="work", bufs=2))
         small = stack.enter_context(tc.tile_pool(name="small", bufs=4))
 
-        w4_codes, w4_planes = load_weight(nc, keep, W4_words, W4_scales, HID, "w4")
-        w5_codes, w5_planes = load_weight(nc, keep, W5_words, W5_scales, DOUT, "w5")
+        w4_planes = load_scale_planes(nc, keep, W4_scales, HID, "w4_planes")
+        w5_planes = load_scale_planes(nc, keep, W5_scales, DOUT, "w5_planes")
         x_rows = keep.tile([P, TOKEN_TILES, HID], BF16, name="x_rows")
         for m in range(TOKEN_TILES):
             nc.sync.dma_start(out=x_rows[:, m, :], in_=h3[m * P : (m + 1) * P, :])
+        w4_codes = keep.tile([P, PASSES, HID], I32, name="w4_codes", align_bytes=64)
         for c in range(HID // N_TILE):
-            load_weight_columns(nc, w4_codes, W4_words, slice(c * N_TILE, (c + 1) * N_TILE))
+            load_words(nc, w4_codes, W4_words, slice(c * N_TILE, (c + 1) * N_TILE))
+        w5_codes = keep.tile([P, PASSES, DOUT], I32, name="w5_codes", align_bytes=64)
         for c in range(DOUT // N_TILE):
-            load_weight_columns(nc, w5_codes, W5_words, slice(c * N_TILE, (c + 1) * N_TILE))
+            load_words(nc, w5_codes, W5_words, slice(c * N_TILE, (c + 1) * N_TILE))
         b4_all = keep.tile([P, HID], BF16, name="b4_all")
         nc.scalar.dma_start(out=b4_all[:], in_=b4.partition_broadcast(P))
         b5_all = keep.tile([P, DOUT], BF16, name="b5_all")
@@ -127,23 +128,24 @@ def tile_matchingnet_pa_kernel(tc, h3, W4_words, W4_scales, b4, W5_words, W5_sca
 
         ident = keep.tile([P, P], F32, name="ident")
         make_identity(nc, ident[:])
-        fold = keep.tile([P, FOLD_REPEAT, GROUP_TILES * SIDE], F32, name="fold")
+        fold = keep.tile([P, FOLD_REPEAT, SIDE], F32, name="fold")
         nc.vector.tensor_reduce(
-            out=fold[:, 0, :], in_=ident[:].rearrange("p (x c) -> p c x", x=BLOCK_ROWS), axis=AXIS.X, op=ALU.add
+            out=fold[:, 0, :], in_=ident[:].rearrange("p (x y) -> p y x", x=BLOCK_ROWS), axis=AXIS.X, op=ALU.add
         )
-        nc.vector.tensor_copy(
-            out=fold[:, 1:, :], in_=fold[:, 0:1, :].to_broadcast([P, FOLD_REPEAT - 1, GROUP_TILES * SIDE])
-        )
+        nc.vector.tensor_copy(out=fold[:, 1:, :], in_=fold[:, 0:1, :].to_broadcast([P, FOLD_REPEAT - 1, SIDE]))
         one = keep.tile([P, 1], F32, name="one")
         nc.vector.memset(one[:], 1.0)
 
-        with tc.psum_pool(name="psum_t", bufs=2) as psum_t, tc.psum_pool(name="psum_acc", bufs=6) as psum_acc:
-            x_codes = keep.tile([P, TOKEN_TILES, PASSES, P], I32, name="x_codes", align_bytes=64)
-            x_planes = keep.tile([P, TOKEN_TILES, PASSES, P], U8, name="x_planes", align_bytes=64)
-            h_codes = keep.tile([P, PASSES, TOKEN_TILES, P], I32, name="h_codes", align_bytes=64)
-            h_planes = keep.tile([P, PASSES, TOKEN_TILES, P], U8, name="h_planes", align_bytes=64)
-            h4 = keep.tile([P, TOKEN_TILES, HID], BF16, name="h4")
+        x_codes = keep.tile([P, TOKEN_TILES, PASSES, P], I32, name="x_codes", align_bytes=64)
+        x_planes = keep.tile([P, TOKEN_TILES, PASSES, P], U8, name="x_planes", align_bytes=64)
+        h_codes = keep.tile([P, PASSES, TOKEN_TILES, P], I32, name="h_codes", align_bytes=64)
+        h_planes = keep.tile([P, PASSES, TOKEN_TILES, P], U8, name="h_planes", align_bytes=64)
+        h4 = keep.tile([P, TOKEN_TILES, HID], BF16, name="h4")
+        z = keep.tile([P, TOKEN_TILES, DOUT], F32, name="z")
+        tail = keep.tile([P, TOKEN_TILES, DOUT], F32, name="tail")
+        kern = [keep.tile([P, SIDE, SIDE], F32, name="kern%d" % m) for m in range(TOKEN_TILES)]
 
+        with tc.psum_pool(name="psum_t", bufs=2) as psum_t, tc.psum_pool(name="psum_acc", bufs=6) as psum_acc:
             for m in range(TOKEN_TILES):
                 grouped = work.tile([P, PASSES, P, PACK], BF16, tag="grouped", align_bytes=64)
                 for g in range(PASSES):
@@ -191,8 +193,6 @@ def tile_matchingnet_pa_kernel(tc, h3, W4_words, W4_scales, b4, W5_words, W5_sca
                     quantise_h4(c - 1)
             quantise_h4(PASSES - 1)
 
-            z = keep.tile([P, TOKEN_TILES, DOUT], F32, name="z")
-            tail = keep.tile([P, TOKEN_TILES, DOUT], F32, name="tail")
             for m in range(TOKEN_TILES):
                 for c in range(DOUT // N_TILE):
                     cols = slice(c * N_TILE, (c + 1) * N_TILE)
@@ -200,8 +200,8 @@ def tile_matchingnet_pa_kernel(tc, h3, W4_words, W4_scales, b4, W5_words, W5_sca
                     mx_product(
                         nc,
                         acc[:],
-                        [h_codes[:, k, m, :] for k in range(PASSES)],
-                        [h_planes[:, k, m, :] for k in range(PASSES)],
+                        [h_codes[:, g, m, :] for g in range(PASSES)],
+                        [h_planes[:, g, m, :] for g in range(PASSES)],
                         w5_codes,
                         w5_planes,
                         cols,
@@ -209,86 +209,79 @@ def tile_matchingnet_pa_kernel(tc, h3, W4_words, W4_scales, b4, W5_words, W5_sca
                     nc.vector.tensor_tensor(out=z[:, m, cols], in0=acc[:], in1=b5_all[:, cols], op=ALU.add)
                 nc.scalar.activation(out=tail[:, m, :], in_=z[:, m, :], func=ACT.Abs)
                 nc.scalar.activation(out=tail[:, m, :], in_=tail[:, m, :], func=ACT.Exp, scale=-1.0)
-                nc.gpsimd.tensor_scalar(out=z[:, m, :], in0=z[:, m, :], scalar1=0.0, scalar2=0.0, op0=ALU.max, op1=ALU.add)
-            kern = []
-            kern_t = []
-            for g in range(GROUPS):
-                kern.append(keep.tile([P, SIDE, GROUP_TILES, SIDE], F32, name="kern%d" % g))
-                kern_t.append(keep.tile([P, SIDE, GROUP_TILES, SIDE], F32, name="kern_t%d" % g))
-                for t in range(GROUP_TILES):
-                    m = GROUP_TILES * g + t
-                    nc.scalar.activation(out=tail[:, m, :], in_=tail[:, m, :], func=ACT.Ln, bias=one[:])
-                    nc.vector.tensor_tensor(
-                        out=kern[g][:, :, t, :],
-                        in0=z[:, m, :].rearrange("p (i j) -> p i j", j=SIDE),
-                        in1=tail[:, m, :].rearrange("p (i j) -> p i j", j=SIDE),
-                        op=ALU.add,
-                    )
+                nc.gpsimd.tensor_scalar(
+                    out=z[:, m, :], in0=z[:, m, :], scalar1=0.0, scalar2=0.0, op0=ALU.max, op1=ALU.add
+                )
+            for m in range(TOKEN_TILES):
+                nc.scalar.activation(out=tail[:, m, :], in_=tail[:, m, :], func=ACT.Ln, bias=one[:])
+                nc.vector.tensor_tensor(
+                    out=kern[m][:].rearrange("p i j -> p (i j)"), in0=z[:, m, :], in1=tail[:, m, :], op=ALU.add
+                )
 
         psum_s = stack.enter_context(tc.psum_pool(name="psum_s", bufs=3))
-        row = []
-        col = []
-        scaled = []
-        for g in range(GROUPS):
-            row.append(keep.tile([P, GROUP_TILES, SIDE], F32, name="row%d" % g))
-            col.append(keep.tile([P, GROUP_TILES, SIDE], F32, name="col%d" % g))
-            scaled.append(keep.tile([P, SIDE, GROUP_TILES, SIDE], F32, name="scaled%d" % g))
-            nc.vector.memset(row[g][:], 1.0)
-            nc.vector.memset(col[g][:], 1.0)
+        kern_t = [keep.tile([P, SIDE, SIDE], F32, name="kern_t%d" % m) for m in range(TOKEN_TILES)]
+        scaled = [keep.tile([P, SIDE, SIDE], F32, name="scaled%d" % m) for m in range(TOKEN_TILES)]
+        row = [keep.tile([P, SIDE], F32, name="row%d" % m) for m in range(TOKEN_TILES)]
+        col = [keep.tile([P, SIDE], F32, name="col%d" % m) for m in range(TOKEN_TILES)]
+        for m in range(TOKEN_TILES):
+            nc.vector.memset(row[m][:], 1.0)
+            nc.vector.memset(col[m][:], 1.0)
 
         steps = []
         for it in range(ROUNDS):
-            steps.extend((g, kern[g], row[g], col[g]) for g in range(GROUPS))
-            steps.extend((g, kern_t[g], col[g], row[g]) for g in range(GROUPS))
+            steps.extend((m, kern[m], row[m], col[m]) for m in range(TOKEN_TILES))
+            steps.extend((m, kern_t[m], col[m], row[m]) for m in range(TOKEN_TILES))
+        steps.extend((m, kern[m], row[m], None) for m in range(TOKEN_TILES))
+        sums = len(steps) - TOKEN_TILES
 
         across = {}
         back = {}
         with tc.manual_schedule():
-            for n in range(len(steps) + 3):
-                if 0 <= n - 1 < len(steps):
+            for n in range(len(steps)):
+                m, mat, factor = steps[n][0:3]
+                product = scaled[m]
+                if n < sums:
+                    across[n] = psum_s.tile([P, P], F32, name="across", tag="across")
+                if n < TOKEN_TILES:
+                    product = mat
+                else:
+                    scale_rows_on_scalar(nc, product, mat, factor, SIDE - SCALAR_ROWS, SIDE)
+                if 0 <= n - 1 < sums:
                     across_sb = small.tile([P, P], F32, tag="across_sb")
                     nc.scalar.copy(out=across_sb[:], in_=across[n - 1][:])
-                for piece in range(PIECES):
-                    if piece == 0 and 0 <= n - 3:
-                        inverse = small.tile([P, GROUP_TILES, SIDE], F32, tag="inverse")
-                        nc.vector.reciprocal(out=inverse[:].rearrange("p t y -> p (t y)"), in_=back[n - 3][:, 0 : GROUP_TILES * SIDE])
-                    if piece == 1 and 0 <= n - 3:
-                        renewed = steps[n - 3][3]
-                        nc.vector.scalar_tensor_tensor(
-                            out=renewed[:], in0=renewed[:], scalar=1.0 / EPS, in1=inverse[:], op0=ALU.mult, op1=ALU.min
-                        )
-                    if n < len(steps):
-                        g, mat, scale = steps[n][0:3]
-                        if piece == 0:
-                            across[n] = psum_s.tile([P, P], F32, name="across", tag="across")
-                        if n < GROUPS:
-                            add_up_piece(nc, across[n], ident, mat, piece)
-                            rows = slice(piece * PIECE_ROWS, (piece + 1) * PIECE_ROWS)
-                            nc.vector.tensor_copy(
-                                out=kern_t[g][:, rows, :, :], in_=mat[:, :, :, rows].rearrange("p i t j -> p j t i")
-                            )
-                        else:
-                            scale_piece(nc, scaled[g], mat, scale, piece)
-                            add_up_piece(nc, across[n], ident, scaled[g], piece)
-                if 0 <= n - 1 < len(steps):
-                    back[n - 1] = psum_s.tile([P, FOLD_REPEAT * GROUP_TILES * SIDE], F32, name="back", tag="back")
-                    nc.tensor.matmul(
-                        out=back[n - 1][:], lhsT=across_sb[:], rhs=fold[:].rearrange("p r c -> p (r c)"), start=True, stop=True
-                    )
 
-            for g in range(GROUPS):
-                for piece in range(PIECES):
-                    scale_piece(nc, scaled[g], kern[g], row[g], piece)
-                result = z[:, GROUP_TILES * g : GROUP_TILES * (g + 1), :].rearrange("p t (i j) -> p t i j", j=SIDE)
-                nc.vector.tensor_tensor(
-                    out=result.rearrange("p t i j -> p i t j"),
-                    in0=scaled[g][:],
-                    in1=col[g][:].unsqueeze(1).to_broadcast([P, SIDE, GROUP_TILES, SIDE]),
-                    op=ALU.mult,
-                )
-                for t in range(GROUP_TILES):
-                    m = GROUP_TILES * g + t
-                    nc.sync.dma_start(
-                        out=out[m * P : (m + 1) * P, :, :].rearrange("b i j -> b (i j)"),
-                        in_=result[:, t, :, :].rearrange("p i j -> p (i j)"),
+                if 0 <= n - 3 < sums:
+                    inverse = small.tile([P, SIDE], F32, tag="inverse")
+                    nc.vector.reciprocal(out=inverse[:], in_=back[n - 3][:, 0:SIDE])
+                if n < TOKEN_TILES:
+                    nc.vector.tensor_copy(out=kern_t[m][:, 0:HALF, :], in_=mat[:, :, 0:HALF].rearrange("p i j -> p j i"))
+                else:
+                    scale_rows(nc, product, mat, factor, 0, HALF)
+                if n < sums:
+                    add_up(nc, across[n], ident, product, 0, HALF)
+
+                if 0 <= n - 3 < sums:
+                    renewed = steps[n - 3][3]
+                    nc.vector.scalar_tensor_tensor(
+                        out=renewed[:], in0=renewed[:], scalar=1.0 / EPS, in1=inverse[:], op0=ALU.mult, op1=ALU.min
                     )
+                if n < TOKEN_TILES:
+                    nc.vector.tensor_copy(
+                        out=kern_t[m][:, HALF:SIDE, :], in_=mat[:, :, HALF:SIDE].rearrange("p i j -> p j i")
+                    )
+                else:
+                    scale_rows(nc, product, mat, factor, HALF, SIDE - SCALAR_ROWS)
+                if n < sums:
+                    add_up(nc, across[n], ident, product, HALF, SIDE)
+
+                if 0 <= n - 1 < sums:
+                    back[n - 1] = psum_s.tile([P, FOLD_REPEAT * SIDE], F32, name="back", tag="back")
+                    nc.tensor.matmul(
+                        out=back[n - 1][:], lhsT=across_sb[:], rhs=fold[:].rearrange("p r y -> p (r y)"), start=True, stop=True
+                    )
+                if n >= sums:
+                    result = z[:, m, :].rearrange("p (i j) -> p i j", j=SIDE)
+                    nc.vector.tensor_tensor(
+                        out=result, in0=product[:], in1=col[m][:].unsqueeze(1).to_broadcast([P, SIDE, SIDE]), op=ALU.mult
+                    )
+                    nc.sync.dma_start(out=out[m * P : (m + 1) * P, :, :].rearrange("b i j -> b (i j)"), in_=z[:, m, :])

@@ -25,6 +25,7 @@ DOUT = SIDE * SIDE
 N_TILE = 512
 SLOPE = 0.01
 EPS = 1e-8
+Z_LINEAR = 30.0
 ROUNDS = 10
 BLOCK_ROWS = P // SIDE
 HALF = SIDE // 2
@@ -135,6 +136,8 @@ def tile_matchingnet_pa_kernel(tc, h3, W4_words, W4_scales, b4, W5_words, W5_sca
         nc.vector.tensor_copy(out=fold[:, 1:, :], in_=fold[:, 0:1, :].to_broadcast([P, FOLD_REPEAT - 1, SIDE]))
         one = keep.tile([P, 1], F32, name="one")
         nc.vector.memset(one[:], 1.0)
+        ln_first = keep.tile([P, 1], F32, name="ln_first")
+        nc.scalar.activation(out=ln_first[:], in_=one[:], func=ACT.Ln)
 
         x_codes = keep.tile([P, TOKEN_TILES, PASSES, P], I32, name="x_codes", align_bytes=64)
         x_planes = keep.tile([P, TOKEN_TILES, PASSES, P], U8, name="x_planes", align_bytes=64)
@@ -171,9 +174,9 @@ def tile_matchingnet_pa_kernel(tc, h3, W4_words, W4_scales, b4, W5_words, W5_sca
                 )
                 pre = work.tile([P, N_TILE], F32, tag="pre", bufs=3)
                 nc.vector.tensor_tensor(out=pre[:], in0=acc[:], in1=b4_all[:, cols], op=ALU.add)
-                low = work.tile([P, N_TILE], F32, tag="low", bufs=3)
-                nc.gpsimd.tensor_scalar(out=low[:], in0=pre[:], scalar1=SLOPE, scalar2=0.0, op0=ALU.mult, op1=ALU.add)
-                nc.vector.tensor_tensor(out=h4[:, m, cols], in0=pre[:], in1=low[:], op=ALU.max)
+                nc.vector.scalar_tensor_tensor(
+                    out=h4[:, m, cols], in0=pre[:], scalar=SLOPE, in1=pre[:], op0=ALU.mult, op1=ALU.max
+                )
 
             def quantise_h4(g):
                 grouped = work.tile([P, TOKEN_TILES, P, PACK], BF16, tag="grouped", align_bytes=64)
@@ -207,15 +210,13 @@ def tile_matchingnet_pa_kernel(tc, h3, W4_words, W4_scales, b4, W5_words, W5_sca
                         cols,
                     )
                     nc.vector.tensor_tensor(out=z[:, m, cols], in0=acc[:], in1=b5_all[:, cols], op=ALU.add)
-                nc.scalar.activation(out=tail[:, m, :], in_=z[:, m, :], func=ACT.Abs)
-                nc.scalar.activation(out=tail[:, m, :], in_=tail[:, m, :], func=ACT.Exp, scale=-1.0)
-                nc.gpsimd.tensor_scalar(
-                    out=z[:, m, :], in0=z[:, m, :], scalar1=0.0, scalar2=0.0, op0=ALU.max, op1=ALU.add
+                nc.vector.tensor_scalar(
+                    out=tail[:, m, :], in0=z[:, m, :], scalar1=Z_LINEAR, scalar2=None, op0=ALU.min
                 )
-            for m in range(TOKEN_TILES):
+                nc.scalar.activation(out=tail[:, m, :], in_=tail[:, m, :], func=ACT.Exp)
                 nc.scalar.activation(out=tail[:, m, :], in_=tail[:, m, :], func=ACT.Ln, bias=one[:])
                 nc.vector.tensor_tensor(
-                    out=kern[m][:].rearrange("p i j -> p (i j)"), in0=z[:, m, :], in1=tail[:, m, :], op=ALU.add
+                    out=kern[m][:].rearrange("p i j -> p (i j)"), in0=z[:, m, :], in1=tail[:, m, :], op=ALU.max
                 )
 
         psum_s = stack.enter_context(tc.psum_pool(name="psum_s", bufs=3))

@@ -28,9 +28,10 @@ EPS = 1e-8
 Z_LINEAR = 30.0
 ROUNDS = 10
 BLOCK_ROWS = P // SIDE
-HALF = SIDE // 2
-SCALAR_ROWS = BLOCK_ROWS
-FOLD_REPEAT = 6
+FIRST = 2 * BLOCK_ROWS
+SCALAR_ROWS = 3 * BLOCK_ROWS
+VECTOR_ROWS = SIDE - SCALAR_ROWS
+FOLD_REPEAT = 5
 
 
 def load_scale_planes(nc, keep, scales, n_cols, name):
@@ -95,7 +96,7 @@ def scale_rows_on_scalar(nc, scaled, mat, factor, first, last):
 def add_up(nc, across, ident, scaled, first, last):
     for b in range(first // BLOCK_ROWS, last // BLOCK_ROWS):
         nc.tensor.matmul(
-            out=across[:],
+            out=across,
             lhsT=scaled[:, b * BLOCK_ROWS : (b + 1) * BLOCK_ROWS, :].rearrange("p x y -> p (x y)"),
             rhs=ident[:],
             is_transpose=True,
@@ -219,7 +220,7 @@ def tile_matchingnet_pa_kernel(tc, h3, W4_words, W4_scales, b4, W5_words, W5_sca
                     out=kern[m][:].rearrange("p i j -> p (i j)"), in0=z[:, m, :], in1=tail[:, m, :], op=ALU.max
                 )
 
-        psum_s = stack.enter_context(tc.psum_pool(name="psum_s", bufs=3))
+        psum_s = stack.enter_context(tc.psum_pool(name="psum_s", bufs=4))
         kern_t = [keep.tile([P, SIDE, SIDE], F32, name="kern_t%d" % m) for m in range(TOKEN_TILES)]
         scaled = [keep.tile([P, SIDE, SIDE], F32, name="scaled%d" % m) for m in range(TOKEN_TILES)]
         row = [keep.tile([P, SIDE], F32, name="row%d" % m) for m in range(TOKEN_TILES)]
@@ -241,45 +242,50 @@ def tile_matchingnet_pa_kernel(tc, h3, W4_words, W4_scales, b4, W5_words, W5_sca
             for n in range(len(steps)):
                 m, mat, factor = steps[n][0:3]
                 product = scaled[m]
-                if n < sums:
-                    across[n] = psum_s.tile([P, P], F32, name="across", tag="across")
-                if n < TOKEN_TILES:
+                first_step = n < TOKEN_TILES
+                if first_step:
                     product = mat
-                else:
-                    scale_rows_on_scalar(nc, product, mat, factor, SIDE - SCALAR_ROWS, SIDE)
+                if n < sums:
+                    across[n] = psum_s.tile([P, N_TILE], F32, name="across", tag="across")[:, 0:P]
+
+                if not first_step:
+                    scale_rows_on_scalar(nc, product, mat, factor, VECTOR_ROWS, VECTOR_ROWS + BLOCK_ROWS)
                 if 0 <= n - 1 < sums:
                     across_sb = small.tile([P, P], F32, tag="across_sb")
-                    nc.scalar.copy(out=across_sb[:], in_=across[n - 1][:])
+                    nc.scalar.copy(out=across_sb[:], in_=across[n - 1])
+                if not first_step:
+                    scale_rows_on_scalar(nc, product, mat, factor, VECTOR_ROWS + BLOCK_ROWS, SIDE)
 
                 if 0 <= n - 3 < sums:
                     inverse = small.tile([P, SIDE], F32, tag="inverse")
                     nc.vector.reciprocal(out=inverse[:], in_=back[n - 3][:, 0:SIDE])
-                if n < TOKEN_TILES:
-                    nc.vector.tensor_copy(out=kern_t[m][:, 0:HALF, :], in_=mat[:, :, 0:HALF].rearrange("p i j -> p j i"))
+                if first_step:
+                    nc.vector.tensor_copy(out=kern_t[m][:, 0:FIRST, :], in_=mat[:, :, 0:FIRST].rearrange("p i j -> p j i"))
                 else:
-                    scale_rows(nc, product, mat, factor, 0, HALF)
+                    scale_rows(nc, product, mat, factor, 0, FIRST)
                 if n < sums:
-                    add_up(nc, across[n], ident, product, 0, HALF)
+                    add_up(nc, across[n], ident, product, 0, FIRST)
+
+                if 0 <= n - 1 < sums:
+                    back[n - 1] = psum_s.tile([P, N_TILE], F32, name="back", tag="back")[:, 0 : FOLD_REPEAT * SIDE]
+                    nc.tensor.matmul(
+                        out=back[n - 1], lhsT=across_sb[:], rhs=fold[:].rearrange("p r y -> p (r y)"), start=True, stop=True
+                    )
 
                 if 0 <= n - 3 < sums:
                     renewed = steps[n - 3][3]
                     nc.vector.scalar_tensor_tensor(
                         out=renewed[:], in0=renewed[:], scalar=1.0 / EPS, in1=inverse[:], op0=ALU.mult, op1=ALU.min
                     )
-                if n < TOKEN_TILES:
+                if first_step:
                     nc.vector.tensor_copy(
-                        out=kern_t[m][:, HALF:SIDE, :], in_=mat[:, :, HALF:SIDE].rearrange("p i j -> p j i")
+                        out=kern_t[m][:, FIRST:SIDE, :], in_=mat[:, :, FIRST:SIDE].rearrange("p i j -> p j i")
                     )
                 else:
-                    scale_rows(nc, product, mat, factor, HALF, SIDE - SCALAR_ROWS)
+                    scale_rows(nc, product, mat, factor, FIRST, VECTOR_ROWS)
                 if n < sums:
-                    add_up(nc, across[n], ident, product, HALF, SIDE)
+                    add_up(nc, across[n], ident, product, FIRST, SIDE)
 
-                if 0 <= n - 1 < sums:
-                    back[n - 1] = psum_s.tile([P, FOLD_REPEAT * SIDE], F32, name="back", tag="back")
-                    nc.tensor.matmul(
-                        out=back[n - 1][:], lhsT=across_sb[:], rhs=fold[:].rearrange("p r y -> p (r y)"), start=True, stop=True
-                    )
                 if n >= sums:
                     result = z[:, m, :].rearrange("p (i j) -> p i j", j=SIDE)
                     nc.vector.tensor_tensor(

@@ -28,10 +28,11 @@ EPS = 1e-8
 Z_LINEAR = 30.0
 ROUNDS = 10
 BLOCK_ROWS = P // SIDE
-FIRST = 2 * BLOCK_ROWS
-SCALAR_ROWS = 3 * BLOCK_ROWS
-VECTOR_ROWS = SIDE - SCALAR_ROWS
-FOLD_REPEAT = 5
+VECTOR_ENDS = (2 * BLOCK_ROWS, 3 * BLOCK_ROWS, 5 * BLOCK_ROWS)
+VECTOR_ROWS = VECTOR_ENDS[-1]
+BLOCK_ORDER = (0, 1, 5, 2, 6, 3, 4, 7)
+FOLD_REPEAT = 2
+CLOCK_COLUMNS = 160
 
 
 def load_scale_planes(nc, keep, scales, n_cols, name):
@@ -93,15 +94,15 @@ def scale_rows_on_scalar(nc, scaled, mat, factor, first, last):
         nc.scalar.activation(out=scaled[:, x, :], in_=mat[:, x, :], func=ACT.Copy, scale=factor[:, x : x + 1])
 
 
-def add_up(nc, across, ident, scaled, first, last):
-    for b in range(first // BLOCK_ROWS, last // BLOCK_ROWS):
+def add_up(nc, across, ident, scaled):
+    for b in BLOCK_ORDER:
         nc.tensor.matmul(
             out=across,
             lhsT=scaled[:, b * BLOCK_ROWS : (b + 1) * BLOCK_ROWS, :].rearrange("p x y -> p (x y)"),
             rhs=ident[:],
             is_transpose=True,
-            start=(b == 0),
-            stop=(b == SIDE // BLOCK_ROWS - 1),
+            start=(b == BLOCK_ORDER[0]),
+            stop=(b == BLOCK_ORDER[-1]),
         )
 
 
@@ -130,11 +131,11 @@ def tile_matchingnet_pa_kernel(tc, h3, W4_words, W4_scales, b4, W5_words, W5_sca
 
         ident = keep.tile([P, P], F32, name="ident")
         make_identity(nc, ident[:])
-        fold = keep.tile([P, FOLD_REPEAT, SIDE], F32, name="fold")
+        fold = keep.tile([P, CLOCK_COLUMNS // SIDE, SIDE], F32, name="fold")
         nc.vector.tensor_reduce(
             out=fold[:, 0, :], in_=ident[:].rearrange("p (x y) -> p y x", x=BLOCK_ROWS), axis=AXIS.X, op=ALU.add
         )
-        nc.vector.tensor_copy(out=fold[:, 1:, :], in_=fold[:, 0:1, :].to_broadcast([P, FOLD_REPEAT - 1, SIDE]))
+        nc.vector.tensor_copy(out=fold[:, 1:, :], in_=fold[:, 0:1, :].to_broadcast([P, CLOCK_COLUMNS // SIDE - 1, SIDE]))
         one = keep.tile([P, 1], F32, name="one")
         nc.vector.memset(one[:], 1.0)
         ln_first = keep.tile([P, 1], F32, name="ln_first")
@@ -220,7 +221,10 @@ def tile_matchingnet_pa_kernel(tc, h3, W4_words, W4_scales, b4, W5_words, W5_sca
                     out=kern[m][:].rearrange("p i j -> p (i j)"), in0=z[:, m, :], in1=tail[:, m, :], op=ALU.max
                 )
 
-        psum_s = stack.enter_context(tc.psum_pool(name="psum_s", bufs=4))
+        psum_across = stack.enter_context(tc.psum_pool(name="psum_across", bufs=4))
+        psum_back = stack.enter_context(tc.psum_pool(name="psum_back", bufs=3))
+        psum_clock = stack.enter_context(tc.psum_pool(name="psum_clock", bufs=1))
+        clock = psum_clock.tile([P, N_TILE], F32, name="clock")
         kern_t = [keep.tile([P, SIDE, SIDE], F32, name="kern_t%d" % m) for m in range(TOKEN_TILES)]
         scaled = [keep.tile([P, SIDE, SIDE], F32, name="scaled%d" % m) for m in range(TOKEN_TILES)]
         row = [keep.tile([P, SIDE], F32, name="row%d" % m) for m in range(TOKEN_TILES)]
@@ -245,46 +249,44 @@ def tile_matchingnet_pa_kernel(tc, h3, W4_words, W4_scales, b4, W5_words, W5_sca
                 first_step = n < TOKEN_TILES
                 if first_step:
                     product = mat
-                if n < sums:
-                    across[n] = psum_s.tile([P, N_TILE], F32, name="across", tag="across")[:, 0:P]
 
-                if not first_step:
-                    scale_rows_on_scalar(nc, product, mat, factor, VECTOR_ROWS, VECTOR_ROWS + BLOCK_ROWS)
-                if 0 <= n - 1 < sums:
+                if 0 <= n - 2 < sums:
                     across_sb = small.tile([P, P], F32, tag="across_sb")
-                    nc.scalar.copy(out=across_sb[:], in_=across[n - 1])
-                if not first_step:
-                    scale_rows_on_scalar(nc, product, mat, factor, VECTOR_ROWS + BLOCK_ROWS, SIDE)
-
-                if 0 <= n - 3 < sums:
-                    inverse = small.tile([P, SIDE], F32, tag="inverse")
-                    nc.vector.reciprocal(out=inverse[:], in_=back[n - 3][:, 0:SIDE])
-                if first_step:
-                    nc.vector.tensor_copy(out=kern_t[m][:, 0:FIRST, :], in_=mat[:, :, 0:FIRST].rearrange("p i j -> p j i"))
-                else:
-                    scale_rows(nc, product, mat, factor, 0, FIRST)
-                if n < sums:
-                    add_up(nc, across[n], ident, product, 0, FIRST)
-
-                if 0 <= n - 1 < sums:
-                    back[n - 1] = psum_s.tile([P, N_TILE], F32, name="back", tag="back")[:, 0 : FOLD_REPEAT * SIDE]
+                    nc.scalar.copy(out=across_sb[:], in_=across[n - 2])
+                    back[n - 2] = psum_back.tile([P, N_TILE], F32, name="back", tag="back")[:, 0 : FOLD_REPEAT * SIDE]
                     nc.tensor.matmul(
-                        out=back[n - 1], lhsT=across_sb[:], rhs=fold[:].rearrange("p r y -> p (r y)"), start=True, stop=True
+                        out=back[n - 2],
+                        lhsT=across_sb[:],
+                        rhs=fold[:].rearrange("p r y -> p (r y)")[:, 0 : FOLD_REPEAT * SIDE],
+                        start=True,
+                        stop=True,
+                    )
+                    nc.tensor.matmul(
+                        out=clock[:, 0:CLOCK_COLUMNS],
+                        lhsT=ident[:],
+                        rhs=fold[:].rearrange("p r y -> p (r y)")[:, 0:CLOCK_COLUMNS],
+                        start=True,
+                        stop=True,
                     )
 
-                if 0 <= n - 3 < sums:
-                    renewed = steps[n - 3][3]
-                    nc.vector.scalar_tensor_tensor(
-                        out=renewed[:], in0=renewed[:], scalar=1.0 / EPS, in1=inverse[:], op0=ALU.mult, op1=ALU.min
-                    )
-                if first_step:
-                    nc.vector.tensor_copy(
-                        out=kern_t[m][:, FIRST:SIDE, :], in_=mat[:, :, FIRST:SIDE].rearrange("p i j -> p j i")
-                    )
-                else:
-                    scale_rows(nc, product, mat, factor, FIRST, VECTOR_ROWS)
+                if not first_step:
+                    scale_rows_on_scalar(nc, product, mat, factor, VECTOR_ROWS, SIDE)
+                for part in range(len(VECTOR_ENDS)):
+                    if not first_step:
+                        scale_rows(nc, product, mat, factor, ((0,) + VECTOR_ENDS)[part], VECTOR_ENDS[part])
+                    elif part == 0:
+                        nc.vector.tensor_copy(out=kern_t[m][:], in_=mat[:].rearrange("p i j -> p j i"))
+                    if part == 0 and 0 <= n - 3 < sums:
+                        inverse = small.tile([P, SIDE], F32, tag="inverse")
+                        nc.vector.reciprocal(out=inverse[:], in_=back[n - 3][:, 0:SIDE])
+                    if part == 1 and 0 <= n - 3 < sums:
+                        renewed = steps[n - 3][3]
+                        nc.vector.scalar_tensor_tensor(
+                            out=renewed[:], in0=renewed[:], scalar=1.0 / EPS, in1=inverse[:], op0=ALU.mult, op1=ALU.min
+                        )
                 if n < sums:
-                    add_up(nc, across[n], ident, product, FIRST, SIDE)
+                    across[n] = psum_across.tile([P, N_TILE], F32, name="across", tag="across")[:, 0:P]
+                    add_up(nc, across[n], ident, product)
 
                 if n >= sums:
                     result = z[:, m, :].rearrange("p (i j) -> p i j", j=SIDE)

@@ -19,20 +19,22 @@ PACK = 4
 K_PASS = P * PACK
 HID = 2048
 PASSES = HID // K_PASS
-TOKEN_TILES = 512 // P
+TOKENS = 512
+TOKEN_TILES = TOKENS // P
 SIDE = 32
 DOUT = SIDE * SIDE
 N_TILE = 512
 SLOPE = 0.01
 EPS = 1e-8
 Z_LINEAR = 30.0
+EARLY_GROUPS = 5
 ROUNDS = 10
 BLOCK_ROWS = P // SIDE
-VECTOR_ENDS = (2 * BLOCK_ROWS, 3 * BLOCK_ROWS, 5 * BLOCK_ROWS)
+VECTOR_ENDS = (6, 14, 18)
 VECTOR_ROWS = VECTOR_ENDS[-1]
-BLOCK_ORDER = (0, 1, 5, 2, 6, 3, 4, 7)
+BLOCK_ORDER = (5, 0, 1, 6, 2, 3, 7, 4)
 FOLD_REPEAT = 2
-CLOCK_COLUMNS = 160
+CLOCK_COLUMNS = 96
 
 
 def load_scale_planes(nc, keep, scales, n_cols, name):
@@ -46,38 +48,31 @@ def load_scale_planes(nc, keep, scales, n_cols, name):
     return planes
 
 
-def load_words(nc, codes, words, cols):
+def load_words(nc, codes, words, c, first, last):
     by_partition = words.rearrange("g p n t -> g p (n t)").bitcast(I32).rearrange("g p n -> p g n")
-    nc.sync.dma_start(out=codes[:, :, cols], in_=by_partition[:, :, cols])
+    nc.sync.dma_start(out=codes[:, first:last, :], in_=by_partition[:, first:last, c * N_TILE : (c + 1) * N_TILE])
 
 
-def flip_pass(nc, psum_t, ident, words, g, grouped):
-    flipped = psum_t.tile([P, 2, P], F32, tag="flipped")
-    for u in range(2):
-        nc.tensor.transpose(flipped[:, u, :], words[:, 256 * g + u : 256 * (g + 1) : 2], ident[:])
-    nc.scalar.copy(
-        out=grouped.rearrange("p r (u e) -> p r u e", e=2),
-        in_=flipped[:].bitcast(BF16).rearrange("p u (r e) -> p r u e", e=2),
+def flip_two_passes(nc, psum, ident, words, g, grouped, copy):
+    flipped = psum.tile([P, N_TILE], F32, name="flipped", tag="bank")[:].rearrange("p (g u r) -> p g u r", g=2, u=2)
+    for i in range(2):
+        for u in range(2):
+            start = 256 * (g + i) + u
+            nc.tensor.transpose(flipped[:, i, u, :], words[:, start : start + 255 : 2], ident[:])
+    copy(
+        out=grouped[:, g : g + 2, :, :].rearrange("p g r t -> p (g r t)").bitcast(F32).rearrange("p (g r u) -> p g r u", g=2, u=2),
+        in_=flipped.rearrange("p g u r -> p g r u"),
     )
 
 
 def quantise(nc, grouped, codes, planes):
-    nc.vector.quantize_mx(
-        out=codes.bitcast(FP8X4), scales=planes, in_=grouped[:].rearrange("p a r t -> p (a r t)")
+    nc.vector.quantize_mx(out=codes.bitcast(FP8X4), scales=planes, in_=grouped.rearrange("p r t -> p (r t)"))
+
+
+def fit_channels(nc, fitted, raw):
+    nc.vector.tensor_copy(
+        out=fitted.rearrange("p (t o i) -> p o t i", t=PACK, i=4), in_=raw.rearrange("p (o i t) -> p o t i", t=PACK, i=4)
     )
-
-
-def mx_product(nc, acc, x_codes, x_planes, w_codes, w_planes, cols):
-    for g in range(PASSES):
-        nc.tensor.matmul_mx(
-            out=acc,
-            lhsT=x_codes[g].bitcast(FP8X4),
-            lhsT_scale=x_planes[g],
-            rhs=w_codes[:, g, cols].bitcast(FP8X4),
-            rhs_scale=w_planes[4 * g : P, cols],
-            start=(g == 0),
-            stop=(g == PASSES - 1),
-        )
 
 
 def scale_rows(nc, scaled, mat, factor, first, last):
@@ -94,10 +89,30 @@ def scale_rows_on_scalar(nc, scaled, mat, factor, first, last):
         nc.scalar.activation(out=scaled[:, x, :], in_=mat[:, x, :], func=ACT.Copy, scale=factor[:, x : x + 1])
 
 
-def add_up(nc, across, ident, scaled):
+def turn_over(copy, mat_t, mat):
+    copy(
+        out=mat_t[:].rearrange("p j (b i) -> p b j i", i=BLOCK_ROWS), in_=mat[:].rearrange("p (b i) j -> p b j i", i=BLOCK_ROWS)
+    )
+
+
+def finish(nc, result, mat_t, factor, first, last):
+    nc.vector.tensor_tensor(
+        out=result[:, first:last, :].rearrange("p i (b j) -> p b i j", j=BLOCK_ROWS),
+        in0=mat_t[:, :, first:last].rearrange("p (b j) i -> p b i j", j=BLOCK_ROWS),
+        in1=factor[:, first:last].unsqueeze(1).unsqueeze(3).to_broadcast([P, SIDE // BLOCK_ROWS, last - first, BLOCK_ROWS]),
+        op=ALU.mult,
+    )
+
+
+def finish_on_scalar(nc, result, mat_t, factor, first, last):
+    for i in range(first, last):
+        nc.scalar.activation(out=result[:, i, :], in_=mat_t[:, :, i], func=ACT.Copy, scale=factor[:, i : i + 1])
+
+
+def add_up(nc, sums, ident, scaled):
     for b in BLOCK_ORDER:
         nc.tensor.matmul(
-            out=across,
+            out=sums,
             lhsT=scaled[:, b * BLOCK_ROWS : (b + 1) * BLOCK_ROWS, :].rearrange("p x y -> p (x y)"),
             rhs=ident[:],
             is_transpose=True,
@@ -113,21 +128,25 @@ def tile_matchingnet_pa_kernel(tc, h3, W4_words, W4_scales, b4, W5_words, W5_sca
         work = stack.enter_context(tc.tile_pool(name="work", bufs=2))
         small = stack.enter_context(tc.tile_pool(name="small", bufs=4))
 
-        w4_planes = load_scale_planes(nc, keep, W4_scales, HID, "w4_planes")
-        w5_planes = load_scale_planes(nc, keep, W5_scales, DOUT, "w5_planes")
+        stack.enter_context(tc.manual_schedule())
+
+        w4_raw_planes = load_scale_planes(nc, keep, W4_scales, HID, "w4_raw_planes")
         x_rows = keep.tile([P, TOKEN_TILES, HID], BF16, name="x_rows")
         for m in range(TOKEN_TILES):
             nc.sync.dma_start(out=x_rows[:, m, :], in_=h3[m * P : (m + 1) * P, :])
-        w4_codes = keep.tile([P, PASSES, HID], I32, name="w4_codes", align_bytes=64)
-        for c in range(HID // N_TILE):
-            load_words(nc, w4_codes, W4_words, slice(c * N_TILE, (c + 1) * N_TILE))
-        w5_codes = keep.tile([P, PASSES, DOUT], I32, name="w5_codes", align_bytes=64)
+        w4_raw = [keep.tile([P, PASSES, N_TILE], I32, name="w4_raw%d" % c) for c in range(PASSES)]
+        for c in range(PASSES):
+            for g in range(0, PASSES, 2):
+                load_words(nc, w4_raw[c], W4_words, c, g, g + 2)
+        w5_planes = load_scale_planes(nc, keep, W5_scales, DOUT, "w5_planes")
+        w5_codes = [keep.tile([P, PASSES, N_TILE], I32, name="w5_codes%d" % c, align_bytes=64) for c in range(DOUT // N_TILE)]
         for c in range(DOUT // N_TILE):
-            load_words(nc, w5_codes, W5_words, slice(c * N_TILE, (c + 1) * N_TILE))
-        b4_all = keep.tile([P, HID], BF16, name="b4_all")
-        nc.scalar.dma_start(out=b4_all[:], in_=b4.partition_broadcast(P))
+            load_words(nc, w5_codes[c], W5_words, c, 0, PASSES)
         b5_all = keep.tile([P, DOUT], BF16, name="b5_all")
-        nc.scalar.dma_start(out=b5_all[:], in_=b5.partition_broadcast(P))
+        nc.sync.dma_start(out=b5_all[:], in_=b5.partition_broadcast(P))
+        b4_raw = keep.tile([P, PASSES, PACK], BF16, name="b4_raw")
+        nc.scalar.dma_start(out=b4_raw[:], in_=b4.rearrange("(c p t) -> p c t", p=P, t=PACK))
+        b4_col = keep.tile([P, PASSES, PACK], F32, name="b4_col")
 
         ident = keep.tile([P, P], F32, name="ident")
         make_identity(nc, ident[:])
@@ -138,90 +157,114 @@ def tile_matchingnet_pa_kernel(tc, h3, W4_words, W4_scales, b4, W5_words, W5_sca
         nc.vector.tensor_copy(out=fold[:, 1:, :], in_=fold[:, 0:1, :].to_broadcast([P, CLOCK_COLUMNS // SIDE - 1, SIDE]))
         one = keep.tile([P, 1], F32, name="one")
         nc.vector.memset(one[:], 1.0)
-        ln_first = keep.tile([P, 1], F32, name="ln_first")
-        nc.scalar.activation(out=ln_first[:], in_=one[:], func=ACT.Ln)
 
-        x_codes = keep.tile([P, TOKEN_TILES, PASSES, P], I32, name="x_codes", align_bytes=64)
-        x_planes = keep.tile([P, TOKEN_TILES, PASSES, P], U8, name="x_planes", align_bytes=64)
-        h_codes = keep.tile([P, PASSES, TOKEN_TILES, P], I32, name="h_codes", align_bytes=64)
-        h_planes = keep.tile([P, PASSES, TOKEN_TILES, P], U8, name="h_planes", align_bytes=64)
-        h4 = keep.tile([P, TOKEN_TILES, HID], BF16, name="h4")
+        w4_codes = [keep.tile([P, PASSES, N_TILE], I32, name="w4_codes%d" % c, align_bytes=64) for c in range(PASSES)]
+        w4_planes = keep.tile([P, HID], U8, name="w4_planes", align_bytes=64)
+        nc.vector.tensor_copy(
+            out=w4_planes[:].rearrange("p (c t m) -> p c t m", c=PASSES, t=PACK),
+            in_=w4_raw_planes[:].rearrange("p (c m t) -> p c t m", c=PASSES, t=PACK),
+        )
+        nc.vector.tensor_copy(out=b4_col[:], in_=b4_raw[:])
+
+        x_codes = keep.tile([P, PASSES, TOKENS], I32, name="x_codes", align_bytes=64)
+        x_planes = keep.tile([P, PASSES, TOKENS], U8, name="x_planes", align_bytes=64)
+        h_codes = keep.tile([P, PASSES, TOKENS], I32, name="h_codes", align_bytes=64)
+        h_planes = keep.tile([P, PASSES, TOKENS], U8, name="h_planes", align_bytes=64)
         z = keep.tile([P, TOKEN_TILES, DOUT], F32, name="z")
-        tail = keep.tile([P, TOKEN_TILES, DOUT], F32, name="tail")
         kern = [keep.tile([P, SIDE, SIDE], F32, name="kern%d" % m) for m in range(TOKEN_TILES)]
 
-        with tc.psum_pool(name="psum_t", bufs=2) as psum_t, tc.psum_pool(name="psum_acc", bufs=6) as psum_acc:
-            for m in range(TOKEN_TILES):
-                grouped = work.tile([P, PASSES, P, PACK], BF16, tag="grouped", align_bytes=64)
+        with tc.psum_pool(name="psum", bufs=8) as psum:
+
+            def quantise_x(m, grouped):
                 for g in range(PASSES):
-                    flip_pass(nc, psum_t, ident, x_rows[:, m, :].bitcast(F32), g, grouped[:, g, :, :])
-                quantise(
-                    nc,
-                    grouped,
-                    x_codes[:, m, :, :].rearrange("p g r -> p (g r)"),
-                    x_planes[:, m, :, :].rearrange("p g r -> p (g r)"),
-                )
+                    toks = slice(m * P, (m + 1) * P)
+                    quantise(nc, grouped[:, g, :, :], x_codes[:, g, toks], x_planes[:, g, toks])
 
-            def layer_1(m, c):
-                cols = slice(c * N_TILE, (c + 1) * N_TILE)
-                acc = psum_acc.tile([P, N_TILE], F32, tag="acc")
-                mx_product(
-                    nc,
-                    acc[:],
-                    [x_codes[:, m, g, :] for g in range(PASSES)],
-                    [x_planes[:, m, g, :] for g in range(PASSES)],
-                    w4_codes,
-                    w4_planes,
-                    cols,
-                )
-                pre = work.tile([P, N_TILE], F32, tag="pre", bufs=3)
-                nc.vector.tensor_tensor(out=pre[:], in0=acc[:], in1=b4_all[:, cols], op=ALU.add)
-                nc.vector.scalar_tensor_tensor(
-                    out=h4[:, m, cols], in0=pre[:], scalar=SLOPE, in1=pre[:], op0=ALU.mult, op1=ALU.max
-                )
-
-            def quantise_h4(g):
-                grouped = work.tile([P, TOKEN_TILES, P, PACK], BF16, tag="grouped", align_bytes=64)
-                for m in range(TOKEN_TILES):
-                    flip_pass(nc, psum_t, ident, h4[:, m, :].bitcast(F32), g, grouped[:, m, :, :])
-                quantise(
-                    nc,
-                    grouped,
-                    h_codes[:, g, :, :].rearrange("p m r -> p (m r)"),
-                    h_planes[:, g, :, :].rearrange("p m r -> p (m r)"),
-                )
-
-            for c in range(PASSES):
-                for m in range(TOKEN_TILES):
-                    layer_1(m, c)
-                if c > 0:
-                    quantise_h4(c - 1)
-            quantise_h4(PASSES - 1)
-
+            x_grouped = []
             for m in range(TOKEN_TILES):
-                for c in range(DOUT // N_TILE):
-                    cols = slice(c * N_TILE, (c + 1) * N_TILE)
-                    acc = psum_acc.tile([P, N_TILE], F32, tag="acc")
-                    mx_product(
-                        nc,
-                        acc[:],
-                        [h_codes[:, g, m, :] for g in range(PASSES)],
-                        [h_planes[:, g, m, :] for g in range(PASSES)],
-                        w5_codes,
-                        w5_planes,
-                        cols,
-                    )
-                    nc.vector.tensor_tensor(out=z[:, m, cols], in0=acc[:], in1=b5_all[:, cols], op=ALU.add)
-                nc.vector.tensor_scalar(
-                    out=tail[:, m, :], in0=z[:, m, :], scalar1=Z_LINEAR, scalar2=None, op0=ALU.min
-                )
-                nc.scalar.activation(out=tail[:, m, :], in_=tail[:, m, :], func=ACT.Exp)
-                nc.scalar.activation(out=tail[:, m, :], in_=tail[:, m, :], func=ACT.Ln, bias=one[:])
-                nc.vector.tensor_tensor(
-                    out=kern[m][:].rearrange("p i j -> p (i j)"), in0=z[:, m, :], in1=tail[:, m, :], op=ALU.max
-                )
+                x_grouped.append(work.tile([P, PASSES, P, PACK], BF16, name="x_grouped", tag="x_grouped", align_bytes=64))
+                words = x_rows[:, m, :].bitcast(F32)
+                flip_two_passes(nc, psum, ident, words, 0, x_grouped[m], nc.scalar.copy)
+                flip_two_passes(nc, psum, ident, words, 2, x_grouped[m], nc.vector.tensor_copy)
+                if m > 0:
+                    quantise_x(m - 1, x_grouped[m - 1])
+            quantise_x(TOKEN_TILES - 1, x_grouped[TOKEN_TILES - 1])
 
-        psum_across = stack.enter_context(tc.psum_pool(name="psum_across", bufs=4))
+            def fit_w4(c):
+                for g in range(PASSES):
+                    fit_channels(nc, w4_codes[c][:, g, :], w4_raw[c][:, g, :])
+
+            def layer_1(c):
+                pre = work.tile([P, PACK, TOKENS], F32, tag="pre")
+                for t in range(PACK):
+                    acc = psum.tile([P, N_TILE], F32, name="acc", tag="bank")
+                    for g in range(PASSES):
+                        nc.tensor.matmul_mx(
+                            out=acc[:],
+                            lhsT=w4_codes[c][:, g, t * P : (t + 1) * P].bitcast(FP8X4),
+                            lhsT_scale=w4_planes[4 * g : P, c * N_TILE + t * P : c * N_TILE + (t + 1) * P],
+                            rhs=x_codes[:, g, :].bitcast(FP8X4),
+                            rhs_scale=x_planes[:, g, :],
+                            start=(g == 0),
+                            stop=(g == PASSES - 1),
+                        )
+                    nc.scalar.activation(out=pre[:, t, :], in_=acc[:], func=ACT.Identity, bias=b4_col[:, c, t : t + 1])
+                halves = []
+                for toks in (slice(0, TOKENS // 2), slice(TOKENS // 2, TOKENS)):
+                    grouped = work.tile([P, TOKENS // 2, PACK], BF16, tag="h_grouped", bufs=4, align_bytes=64)
+                    side_by_side = pre[:, :, toks].rearrange("p t r -> p r t")
+                    nc.vector.scalar_tensor_tensor(
+                        out=grouped[:], in0=side_by_side, scalar=SLOPE, in1=side_by_side, op0=ALU.mult, op1=ALU.max
+                    )
+                    halves.append((grouped, toks))
+                for grouped, toks in halves:
+                    quantise(nc, grouped[:], h_codes[:, c, toks], h_planes[:, c, toks])
+
+            def layer_2(m, c, acc, first, last):
+                for g in range(first, last):
+                    nc.tensor.matmul_mx(
+                        out=acc[:],
+                        lhsT=h_codes[:, g, m * P : (m + 1) * P].bitcast(FP8X4),
+                        lhsT_scale=h_planes[:, g, m * P : (m + 1) * P],
+                        rhs=w5_codes[c][:, g, :].bitcast(FP8X4),
+                        rhs_scale=w5_planes[4 * g : P, c * N_TILE : (c + 1) * N_TILE],
+                        start=(g == 0),
+                        stop=(g == PASSES - 1),
+                    )
+
+            fit_w4(0)
+            fit_w4(1)
+            fit_w4(2)
+            layer_1(0)
+            fit_w4(3)
+            for c in range(1, PASSES):
+                layer_1(c)
+
+            groups = [(m, c) for m in range(TOKEN_TILES) for c in range(DOUT // N_TILE)]
+            accs = []
+            for m, c in groups[:EARLY_GROUPS]:
+                accs.append(psum.tile([P, N_TILE], F32, name="acc", tag="bank"))
+                layer_2(m, c, accs[-1], 0, PASSES - 1)
+
+            def exponential(m, c):
+                cols = slice(c * N_TILE, (c + 1) * N_TILE)
+                part = kern[m][:].rearrange("p i j -> p (i j)")[:, cols]
+                nc.vector.tensor_scalar(out=part, in0=z[:, m, cols], scalar1=Z_LINEAR, scalar2=None, op0=ALU.min)
+                nc.scalar.activation(out=part, in_=part, func=ACT.Exp)
+
+            for k, (m, c) in enumerate(groups):
+                if k < EARLY_GROUPS:
+                    layer_2(m, c, accs[k], PASSES - 1, PASSES)
+                else:
+                    accs.append(psum.tile([P, N_TILE], F32, name="acc", tag="bank"))
+                    layer_2(m, c, accs[k], 0, PASSES)
+                cols = slice(c * N_TILE, (c + 1) * N_TILE)
+                nc.vector.tensor_tensor(out=z[:, m, cols], in0=accs[k][:], in1=b5_all[:, cols], op=ALU.add)
+                if k > 0:
+                    exponential(*groups[k - 1])
+            exponential(*groups[-1])
+
+        psum_sums = stack.enter_context(tc.psum_pool(name="psum_sums", bufs=4))
         psum_back = stack.enter_context(tc.psum_pool(name="psum_back", bufs=3))
         psum_clock = stack.enter_context(tc.psum_pool(name="psum_clock", bufs=1))
         clock = psum_clock.tile([P, N_TILE], F32, name="clock")
@@ -237,60 +280,77 @@ def tile_matchingnet_pa_kernel(tc, h3, W4_words, W4_scales, b4, W5_words, W5_sca
         for it in range(ROUNDS):
             steps.extend((m, kern[m], row[m], col[m]) for m in range(TOKEN_TILES))
             steps.extend((m, kern_t[m], col[m], row[m]) for m in range(TOKEN_TILES))
-        steps.extend((m, kern[m], row[m], None) for m in range(TOKEN_TILES))
-        sums = len(steps) - TOKEN_TILES
-
-        across = {}
+        sums = {}
         back = {}
-        with tc.manual_schedule():
-            for n in range(len(steps)):
+        inverse = {}
+
+        def add_up_step(n, product):
+            sums[n] = psum_sums.tile([P, N_TILE], F32, name="sums", tag="sums")[:, 0:P]
+            add_up(nc, sums[n], ident, product)
+
+        def fold_step(n):
+            sums_sb = small.tile([P, P], F32, name="sums_sb", tag="sums_sb")
+            nc.scalar.copy(out=sums_sb[:], in_=sums[n])
+            back[n] = psum_back.tile([P, N_TILE], F32, name="back", tag="back")[:, 0 : FOLD_REPEAT * SIDE]
+            nc.tensor.matmul(
+                out=back[n],
+                lhsT=sums_sb[:],
+                rhs=fold[:].rearrange("p r y -> p (r y)")[:, 0 : FOLD_REPEAT * SIDE],
+                start=True,
+                stop=True,
+            )
+            nc.tensor.matmul(
+                out=clock[:, 0:CLOCK_COLUMNS],
+                lhsT=ident[:],
+                rhs=fold[:].rearrange("p r y -> p (r y)")[:, 0:CLOCK_COLUMNS],
+                start=True,
+                stop=True,
+            )
+
+        def invert_step(n):
+            inverse[n] = small.tile([P, SIDE], F32, name="inverse", tag="inverse")
+            nc.vector.reciprocal(out=inverse[n][:], in_=back[n][:, 0:SIDE])
+
+        def renew_step(n):
+            renewed = steps[n][3]
+            nc.vector.scalar_tensor_tensor(
+                out=renewed[:], in0=renewed[:], scalar=1.0 / EPS, in1=inverse[n][:], op0=ALU.mult, op1=ALU.min
+            )
+
+        for m in range(TOKEN_TILES):
+            log = kern[m][:].rearrange("p i j -> p (i j)")
+            nc.scalar.activation(out=log, in_=log, func=ACT.Ln, bias=one[:])
+            nc.vector.tensor_tensor(out=log, in0=z[:, m, :], in1=log, op=ALU.max)
+            add_up_step(m, kern[m])
+        fold_step(0)
+        turn_over(nc.scalar.copy, kern_t[0], kern[0])
+        fold_step(1)
+        turn_over(nc.scalar.copy, kern_t[1], kern[1])
+        invert_step(0)
+        turn_over(nc.vector.tensor_copy, kern_t[2], kern[2])
+        renew_step(0)
+        turn_over(nc.vector.tensor_copy, kern_t[3], kern[3])
+
+        starts = (0,) + VECTOR_ENDS[:-1]
+        for n in range(TOKEN_TILES, len(steps) + TOKEN_TILES):
+            if n - 2 < len(steps):
+                fold_step(n - 2)
+            if n < len(steps):
                 m, mat, factor = steps[n][0:3]
-                product = scaled[m]
-                first_step = n < TOKEN_TILES
-                if first_step:
-                    product = mat
-
-                if 0 <= n - 2 < sums:
-                    across_sb = small.tile([P, P], F32, tag="across_sb")
-                    nc.scalar.copy(out=across_sb[:], in_=across[n - 2])
-                    back[n - 2] = psum_back.tile([P, N_TILE], F32, name="back", tag="back")[:, 0 : FOLD_REPEAT * SIDE]
-                    nc.tensor.matmul(
-                        out=back[n - 2],
-                        lhsT=across_sb[:],
-                        rhs=fold[:].rearrange("p r y -> p (r y)")[:, 0 : FOLD_REPEAT * SIDE],
-                        start=True,
-                        stop=True,
-                    )
-                    nc.tensor.matmul(
-                        out=clock[:, 0:CLOCK_COLUMNS],
-                        lhsT=ident[:],
-                        rhs=fold[:].rearrange("p r y -> p (r y)")[:, 0:CLOCK_COLUMNS],
-                        start=True,
-                        stop=True,
-                    )
-
-                if not first_step:
-                    scale_rows_on_scalar(nc, product, mat, factor, VECTOR_ROWS, SIDE)
-                for part in range(len(VECTOR_ENDS)):
-                    if not first_step:
-                        scale_rows(nc, product, mat, factor, ((0,) + VECTOR_ENDS)[part], VECTOR_ENDS[part])
-                    elif part == 0:
-                        nc.vector.tensor_copy(out=kern_t[m][:], in_=mat[:].rearrange("p i j -> p j i"))
-                    if part == 0 and 0 <= n - 3 < sums:
-                        inverse = small.tile([P, SIDE], F32, tag="inverse")
-                        nc.vector.reciprocal(out=inverse[:], in_=back[n - 3][:, 0:SIDE])
-                    if part == 1 and 0 <= n - 3 < sums:
-                        renewed = steps[n - 3][3]
-                        nc.vector.scalar_tensor_tensor(
-                            out=renewed[:], in0=renewed[:], scalar=1.0 / EPS, in1=inverse[:], op0=ALU.mult, op1=ALU.min
-                        )
-                if n < sums:
-                    across[n] = psum_across.tile([P, N_TILE], F32, name="across", tag="across")[:, 0:P]
-                    add_up(nc, across[n], ident, product)
-
-                if n >= sums:
-                    result = z[:, m, :].rearrange("p (i j) -> p i j", j=SIDE)
-                    nc.vector.tensor_tensor(
-                        out=result, in0=product[:], in1=col[m][:].unsqueeze(1).to_broadcast([P, SIDE, SIDE]), op=ALU.mult
-                    )
-                    nc.sync.dma_start(out=out[m * P : (m + 1) * P, :, :].rearrange("b i j -> b (i j)"), in_=z[:, m, :])
+                scale_rows_on_scalar(nc, scaled[m], mat, factor, VECTOR_ROWS, SIDE)
+                scale_rows(nc, scaled[m], mat, factor, starts[0], VECTOR_ENDS[0])
+            if n - 3 < len(steps):
+                invert_step(n - 3)
+            if n < len(steps):
+                scale_rows(nc, scaled[m], mat, factor, starts[1], VECTOR_ENDS[1])
+            if n - 3 < len(steps):
+                renew_step(n - 3)
+            if n < len(steps):
+                scale_rows(nc, scaled[m], mat, factor, starts[2], VECTOR_ENDS[2])
+                add_up_step(n, scaled[m])
+            else:
+                m = n - len(steps)
+                result = z[:, m, :].rearrange("p (i j) -> p i j", j=SIDE)
+                finish_on_scalar(nc, result, scaled[m], row[m], VECTOR_ROWS, SIDE)
+                finish(nc, result, scaled[m], row[m], 0, VECTOR_ROWS)
+                nc.sync.dma_start(out=out[m * P : (m + 1) * P, :, :].rearrange("b i j -> b (i j)"), in_=z[:, m, :])

@@ -30,11 +30,12 @@ Z_LINEAR = 30.0
 EARLY_GROUPS = 5
 ROUNDS = 10
 BLOCK_ROWS = P // SIDE
-VECTOR_ENDS = (6, 14, 18)
+VECTOR_ENDS = (8, 12, 18)
 VECTOR_ROWS = VECTOR_ENDS[-1]
-BLOCK_ORDER = (5, 0, 1, 6, 2, 3, 7, 4)
+BLOCK_ORDER = (0, 1, 5, 2, 6, 3, 4, 7)
 FOLD_REPEAT = 2
-CLOCK_COLUMNS = 96
+CLOCK_RUN = 6
+CLOCK_COLUMNS = 64
 
 
 def load_scale_planes(nc, keep, scales, n_cols, name):
@@ -130,10 +131,11 @@ def tile_matchingnet_pa_kernel(tc, h3, W4_words, W4_scales, b4, W5_words, W5_sca
 
         stack.enter_context(tc.manual_schedule())
 
-        w4_raw_planes = load_scale_planes(nc, keep, W4_scales, HID, "w4_raw_planes")
         x_rows = keep.tile([P, TOKEN_TILES, HID], BF16, name="x_rows")
         for m in range(TOKEN_TILES):
             nc.sync.dma_start(out=x_rows[:, m, :], in_=h3[m * P : (m + 1) * P, :])
+            if m == 0:
+                w4_raw_planes = load_scale_planes(nc, keep, W4_scales, HID, "w4_raw_planes")
         w4_raw = [keep.tile([P, PASSES, N_TILE], I32, name="w4_raw%d" % c) for c in range(PASSES)]
         for c in range(PASSES):
             for g in range(0, PASSES, 2):
@@ -175,24 +177,25 @@ def tile_matchingnet_pa_kernel(tc, h3, W4_words, W4_scales, b4, W5_words, W5_sca
 
         with tc.psum_pool(name="psum", bufs=8) as psum:
 
-            def quantise_x(m, grouped):
-                for g in range(PASSES):
-                    toks = slice(m * P, (m + 1) * P)
-                    quantise(nc, grouped[:, g, :, :], x_codes[:, g, toks], x_planes[:, g, toks])
+            def quantise_x(m, g):
+                toks = slice(m * P, (m + 1) * P)
+                quantise(nc, x_grouped[m][:, g, :, :], x_codes[:, g, toks], x_planes[:, g, toks])
+
+            def fit_w4(c, g):
+                fit_channels(nc, w4_codes[c][:, g, :], w4_raw[c][:, g, :])
 
             x_grouped = []
             for m in range(TOKEN_TILES):
                 x_grouped.append(work.tile([P, PASSES, P, PACK], BF16, name="x_grouped", tag="x_grouped", align_bytes=64))
                 words = x_rows[:, m, :].bitcast(F32)
                 flip_two_passes(nc, psum, ident, words, 0, x_grouped[m], nc.scalar.copy)
-                flip_two_passes(nc, psum, ident, words, 2, x_grouped[m], nc.vector.tensor_copy)
+                flip_two_passes(nc, psum, ident, words, 2, x_grouped[m], nc.vector.tensor_copy if m % 2 else nc.scalar.copy)
                 if m > 0:
-                    quantise_x(m - 1, x_grouped[m - 1])
-            quantise_x(TOKEN_TILES - 1, x_grouped[TOKEN_TILES - 1])
-
-            def fit_w4(c):
-                for g in range(PASSES):
-                    fit_channels(nc, w4_codes[c][:, g, :], w4_raw[c][:, g, :])
+                    for g in range(PASSES):
+                        quantise_x(m - 1, g)
+            for g in range(PASSES):
+                fit_w4(0, g)
+                quantise_x(TOKEN_TILES - 1, g)
 
             def layer_1(c):
                 pre = work.tile([P, PACK, TOKENS], F32, tag="pre")
@@ -232,11 +235,12 @@ def tile_matchingnet_pa_kernel(tc, h3, W4_words, W4_scales, b4, W5_words, W5_sca
                         stop=(g == PASSES - 1),
                     )
 
-            fit_w4(0)
-            fit_w4(1)
-            fit_w4(2)
+            for c in (1, 2):
+                for g in range(PASSES):
+                    fit_w4(c, g)
             layer_1(0)
-            fit_w4(3)
+            for g in range(PASSES):
+                fit_w4(3, g)
             for c in range(1, PASSES):
                 layer_1(c)
 
@@ -264,10 +268,15 @@ def tile_matchingnet_pa_kernel(tc, h3, W4_words, W4_scales, b4, W5_words, W5_sca
                     exponential(*groups[k - 1])
             exponential(*groups[-1])
 
-        psum_sums = stack.enter_context(tc.psum_pool(name="psum_sums", bufs=4))
-        psum_back = stack.enter_context(tc.psum_pool(name="psum_back", bufs=3))
+            clock_run = psum.tile([P, N_TILE], F32, name="clock_run", tag="bank")
+            for m, c in groups[:CLOCK_RUN]:
+                cols = slice(c * N_TILE, (c + 1) * N_TILE)
+                nc.tensor.matmul(out=clock_run[:], lhsT=ident[:], rhs=z[:, m, cols], start=True, stop=True)
+
         psum_clock = stack.enter_context(tc.psum_pool(name="psum_clock", bufs=1))
         clock = psum_clock.tile([P, N_TILE], F32, name="clock")
+        psum_sums = stack.enter_context(tc.psum_pool(name="psum_sums", bufs=4))
+        psum_back = stack.enter_context(tc.psum_pool(name="psum_back", bufs=3))
         kern_t = [keep.tile([P, SIDE, SIDE], F32, name="kern_t%d" % m) for m in range(TOKEN_TILES)]
         scaled = [keep.tile([P, SIDE, SIDE], F32, name="scaled%d" % m) for m in range(TOKEN_TILES)]
         row = [keep.tile([P, SIDE], F32, name="row%d" % m) for m in range(TOKEN_TILES)]
@@ -299,6 +308,8 @@ def tile_matchingnet_pa_kernel(tc, h3, W4_words, W4_scales, b4, W5_words, W5_sca
                 start=True,
                 stop=True,
             )
+
+        def keep_clock():
             nc.tensor.matmul(
                 out=clock[:, 0:CLOCK_COLUMNS],
                 lhsT=ident[:],
@@ -320,37 +331,41 @@ def tile_matchingnet_pa_kernel(tc, h3, W4_words, W4_scales, b4, W5_words, W5_sca
         for m in range(TOKEN_TILES):
             log = kern[m][:].rearrange("p i j -> p (i j)")
             nc.scalar.activation(out=log, in_=log, func=ACT.Ln, bias=one[:])
+            if m == TOKEN_TILES - 1:
+                fold_step(0)
             nc.vector.tensor_tensor(out=log, in0=z[:, m, :], in1=log, op=ALU.max)
             add_up_step(m, kern[m])
-        fold_step(0)
+            keep_clock()
         turn_over(nc.scalar.copy, kern_t[0], kern[0])
         fold_step(1)
         turn_over(nc.scalar.copy, kern_t[1], kern[1])
         invert_step(0)
-        turn_over(nc.vector.tensor_copy, kern_t[2], kern[2])
         renew_step(0)
-        turn_over(nc.vector.tensor_copy, kern_t[3], kern[3])
 
         starts = (0,) + VECTOR_ENDS[:-1]
         for n in range(TOKEN_TILES, len(steps) + TOKEN_TILES):
             if n - 2 < len(steps):
                 fold_step(n - 2)
+                keep_clock()
+            if n - 3 < len(steps):
+                invert_step(n - 3)
             if n < len(steps):
                 m, mat, factor = steps[n][0:3]
                 scale_rows_on_scalar(nc, scaled[m], mat, factor, VECTOR_ROWS, SIDE)
                 scale_rows(nc, scaled[m], mat, factor, starts[0], VECTOR_ENDS[0])
             if n - 3 < len(steps):
-                invert_step(n - 3)
-            if n < len(steps):
-                scale_rows(nc, scaled[m], mat, factor, starts[1], VECTOR_ENDS[1])
-            if n - 3 < len(steps):
                 renew_step(n - 3)
             if n < len(steps):
-                scale_rows(nc, scaled[m], mat, factor, starts[2], VECTOR_ENDS[2])
+                for first, last in zip(starts[1:], VECTOR_ENDS[1:]):
+                    scale_rows(nc, scaled[m], mat, factor, first, last)
                 add_up_step(n, scaled[m])
+                if n - 2 in (2, 3):
+                    turn_over(nc.vector.tensor_copy, kern_t[n - 2], kern[n - 2])
             else:
                 m = n - len(steps)
                 result = z[:, m, :].rearrange("p (i j) -> p i j", j=SIDE)
-                finish_on_scalar(nc, result, scaled[m], row[m], VECTOR_ROWS, SIDE)
-                finish(nc, result, scaled[m], row[m], 0, VECTOR_ROWS)
-                nc.sync.dma_start(out=out[m * P : (m + 1) * P, :, :].rearrange("b i j -> b (i j)"), in_=z[:, m, :])
+                for first in (0, SIDE // 2):
+                    middle, last = first + VECTOR_ROWS // 2, first + SIDE // 2
+                    finish_on_scalar(nc, result, scaled[m], row[m], middle, last)
+                    finish(nc, result, scaled[m], row[m], first, middle)
+                    nc.sync.dma_start(out=out[m * P : (m + 1) * P, first:last, :], in_=result[:, first:last, :])

@@ -30,10 +30,11 @@ Z_LINEAR = 30.0
 EARLY_GROUPS = 5
 ROUNDS = 10
 BLOCK_ROWS = P // SIDE
-VECTOR_ENDS = (8, 12, 18)
+VECTOR_ENDS = (8, 17)
 VECTOR_ROWS = VECTOR_ENDS[-1]
-BLOCK_ORDER = (0, 1, 5, 2, 6, 3, 4, 7)
+BLOCK_ORDER = (0, 1, 5, 6, 2, 3, 4, 7)
 FOLD_REPEAT = 2
+CLOCK_START = 4
 CLOCK_RUN = 6
 CLOCK_COLUMNS = 64
 
@@ -162,10 +163,6 @@ def tile_matchingnet_pa_kernel(tc, h3, W4_words, W4_scales, b4, W5_words, W5_sca
 
         w4_codes = [keep.tile([P, PASSES, N_TILE], I32, name="w4_codes%d" % c, align_bytes=64) for c in range(PASSES)]
         w4_planes = keep.tile([P, HID], U8, name="w4_planes", align_bytes=64)
-        nc.vector.tensor_copy(
-            out=w4_planes[:].rearrange("p (c t m) -> p c t m", c=PASSES, t=PACK),
-            in_=w4_raw_planes[:].rearrange("p (c m t) -> p c t m", c=PASSES, t=PACK),
-        )
         nc.vector.tensor_copy(out=b4_col[:], in_=b4_raw[:])
 
         x_codes = keep.tile([P, PASSES, TOKENS], I32, name="x_codes", align_bytes=64)
@@ -177,6 +174,10 @@ def tile_matchingnet_pa_kernel(tc, h3, W4_words, W4_scales, b4, W5_words, W5_sca
 
         with tc.psum_pool(name="psum", bufs=8) as psum:
 
+            clock_start = psum.tile([P, N_TILE], F32, name="clock_start", tag="bank")
+            for i in range(CLOCK_START):
+                nc.tensor.matmul(out=clock_start[:, 0:P], lhsT=ident[:], rhs=ident[:], start=True, stop=True)
+
             def quantise_x(m, g):
                 toks = slice(m * P, (m + 1) * P)
                 quantise(nc, x_grouped[m][:, g, :, :], x_codes[:, g, toks], x_planes[:, g, toks])
@@ -184,15 +185,23 @@ def tile_matchingnet_pa_kernel(tc, h3, W4_words, W4_scales, b4, W5_words, W5_sca
             def fit_w4(c, g):
                 fit_channels(nc, w4_codes[c][:, g, :], w4_raw[c][:, g, :])
 
+            def fit_w4_planes(c):
+                cols = slice(c * N_TILE, (c + 1) * N_TILE)
+                nc.vector.tensor_copy(
+                    out=w4_planes[:, cols].rearrange("p (t m) -> p t m", t=PACK),
+                    in_=w4_raw_planes[:, cols].rearrange("p (m t) -> p t m", t=PACK),
+                )
+
+            fit_w4_planes(0)
             x_grouped = []
             for m in range(TOKEN_TILES):
                 x_grouped.append(work.tile([P, PASSES, P, PACK], BF16, name="x_grouped", tag="x_grouped", align_bytes=64))
                 words = x_rows[:, m, :].bitcast(F32)
                 flip_two_passes(nc, psum, ident, words, 0, x_grouped[m], nc.scalar.copy)
-                flip_two_passes(nc, psum, ident, words, 2, x_grouped[m], nc.vector.tensor_copy if m % 2 else nc.scalar.copy)
                 if m > 0:
                     for g in range(PASSES):
                         quantise_x(m - 1, g)
+                flip_two_passes(nc, psum, ident, words, 2, x_grouped[m], nc.vector.tensor_copy if m % 2 else nc.scalar.copy)
             for g in range(PASSES):
                 fit_w4(0, g)
                 quantise_x(TOKEN_TILES - 1, g)
@@ -235,12 +244,15 @@ def tile_matchingnet_pa_kernel(tc, h3, W4_words, W4_scales, b4, W5_words, W5_sca
                         stop=(g == PASSES - 1),
                     )
 
-            for c in (1, 2):
+            def fit_w4_chunk(c):
+                fit_w4_planes(c)
                 for g in range(PASSES):
                     fit_w4(c, g)
+
+            fit_w4_chunk(1)
+            fit_w4_chunk(2)
             layer_1(0)
-            for g in range(PASSES):
-                fit_w4(3, g)
+            fit_w4_chunk(3)
             for c in range(1, PASSES):
                 layer_1(c)
 
@@ -333,11 +345,11 @@ def tile_matchingnet_pa_kernel(tc, h3, W4_words, W4_scales, b4, W5_words, W5_sca
             nc.scalar.activation(out=log, in_=log, func=ACT.Ln, bias=one[:])
             if m == TOKEN_TILES - 1:
                 fold_step(0)
+                fold_step(1)
             nc.vector.tensor_tensor(out=log, in0=z[:, m, :], in1=log, op=ALU.max)
             add_up_step(m, kern[m])
             keep_clock()
         turn_over(nc.scalar.copy, kern_t[0], kern[0])
-        fold_step(1)
         turn_over(nc.scalar.copy, kern_t[1], kern[1])
         invert_step(0)
         renew_step(0)

@@ -30,13 +30,13 @@ Z_LINEAR = 30.0
 EARLY_GROUPS = 5
 ROUNDS = 10
 BLOCK_ROWS = P // SIDE
-VECTOR_ENDS = (8, 17)
+VECTOR_ENDS = (8, 12, 18)
 VECTOR_ROWS = VECTOR_ENDS[-1]
-BLOCK_ORDER = (0, 1, 5, 6, 2, 3, 4, 7)
+BLOCK_ORDER = (0, 1, 5, 2, 6, 3, 4, 7)
 FOLD_REPEAT = 2
 CLOCK_START = 4
 CLOCK_RUN = 6
-CLOCK_COLUMNS = 64
+CLOCK_COLUMNS = 96
 
 
 def load_scale_planes(nc, keep, scales, n_cols, name):

@@ -36,7 +36,7 @@ BLOCK_ORDER = (0, 1, 5, 2, 6, 3, 4, 7)
 FOLD_REPEAT = 2
 CLOCK_START = 4
 CLOCK_RUN = 6
-CLOCK_COLUMNS = 96
+CLOCK_COLUMNS = 80
 
 
 def load_scale_planes(nc, keep, scales, n_cols, name):
@@ -153,11 +153,11 @@ def tile_matchingnet_pa_kernel(tc, h3, W4_words, W4_scales, b4, W5_words, W5_sca
 
         ident = keep.tile([P, P], F32, name="ident")
         make_identity(nc, ident[:])
-        fold = keep.tile([P, CLOCK_COLUMNS // SIDE, SIDE], F32, name="fold")
+        fold = keep.tile([P, FOLD_REPEAT, SIDE], F32, name="fold")
         nc.vector.tensor_reduce(
             out=fold[:, 0, :], in_=ident[:].rearrange("p (x y) -> p y x", x=BLOCK_ROWS), axis=AXIS.X, op=ALU.add
         )
-        nc.vector.tensor_copy(out=fold[:, 1:, :], in_=fold[:, 0:1, :].to_broadcast([P, CLOCK_COLUMNS // SIDE - 1, SIDE]))
+        nc.vector.tensor_copy(out=fold[:, 1:, :], in_=fold[:, 0:1, :].to_broadcast([P, FOLD_REPEAT - 1, SIDE]))
         one = keep.tile([P, 1], F32, name="one")
         nc.vector.memset(one[:], 1.0)
 
@@ -316,16 +316,16 @@ def tile_matchingnet_pa_kernel(tc, h3, W4_words, W4_scales, b4, W5_words, W5_sca
             nc.tensor.matmul(
                 out=back[n],
                 lhsT=sums_sb[:],
-                rhs=fold[:].rearrange("p r y -> p (r y)")[:, 0 : FOLD_REPEAT * SIDE],
+                rhs=fold[:].rearrange("p r y -> p (r y)"),
                 start=True,
                 stop=True,
             )
 
-        def keep_clock():
+        def keep_clock(columns):
             nc.tensor.matmul(
-                out=clock[:, 0:CLOCK_COLUMNS],
+                out=clock[:, 0:columns],
                 lhsT=ident[:],
-                rhs=fold[:].rearrange("p r y -> p (r y)")[:, 0:CLOCK_COLUMNS],
+                rhs=ident[:, 0:columns],
                 start=True,
                 stop=True,
             )
@@ -348,36 +348,40 @@ def tile_matchingnet_pa_kernel(tc, h3, W4_words, W4_scales, b4, W5_words, W5_sca
                 fold_step(1)
             nc.vector.tensor_tensor(out=log, in0=z[:, m, :], in1=log, op=ALU.max)
             add_up_step(m, kern[m])
-            keep_clock()
+            keep_clock(P)
         turn_over(nc.scalar.copy, kern_t[0], kern[0])
         turn_over(nc.scalar.copy, kern_t[1], kern[1])
         invert_step(0)
         renew_step(0)
 
         starts = (0,) + VECTOR_ENDS[:-1]
-        for n in range(TOKEN_TILES, len(steps) + TOKEN_TILES):
+        for n in range(TOKEN_TILES, len(steps)):
+            fold_step(n - 2)
+            keep_clock(P if n < 3 * TOKEN_TILES else CLOCK_COLUMNS)
+            invert_step(n - 3)
+            m, mat, factor = steps[n][0:3]
+            scale_rows_on_scalar(nc, scaled[m], mat, factor, VECTOR_ROWS, SIDE)
+            scale_rows(nc, scaled[m], mat, factor, starts[0], VECTOR_ENDS[0])
+            renew_step(n - 3)
+            for first, last in zip(starts[1:], VECTOR_ENDS[1:]):
+                scale_rows(nc, scaled[m], mat, factor, first, last)
+            add_up_step(n, scaled[m])
+            if n - 2 in (2, 3):
+                turn_over(nc.vector.tensor_copy, kern_t[n - 2], kern[n - 2])
+
+        def finish_half(m, first):
+            result = z[:, m, :].rearrange("p (i j) -> p i j", j=SIDE)
+            middle, last = first + VECTOR_ROWS // 2, first + SIDE // 2
+            finish_on_scalar(nc, result, scaled[m], row[m], middle, last)
+            finish(nc, result, scaled[m], row[m], first, middle)
+            nc.sync.dma_start(out=out[m * P : (m + 1) * P, first:last, :], in_=result[:, first:last, :])
+
+        for m in range(TOKEN_TILES):
+            n = len(steps) + m
             if n - 2 < len(steps):
                 fold_step(n - 2)
-                keep_clock()
+            finish_half(m, 0)
             if n - 3 < len(steps):
                 invert_step(n - 3)
-            if n < len(steps):
-                m, mat, factor = steps[n][0:3]
-                scale_rows_on_scalar(nc, scaled[m], mat, factor, VECTOR_ROWS, SIDE)
-                scale_rows(nc, scaled[m], mat, factor, starts[0], VECTOR_ENDS[0])
-            if n - 3 < len(steps):
                 renew_step(n - 3)
-            if n < len(steps):
-                for first, last in zip(starts[1:], VECTOR_ENDS[1:]):
-                    scale_rows(nc, scaled[m], mat, factor, first, last)
-                add_up_step(n, scaled[m])
-                if n - 2 in (2, 3):
-                    turn_over(nc.vector.tensor_copy, kern_t[n - 2], kern[n - 2])
-            else:
-                m = n - len(steps)
-                result = z[:, m, :].rearrange("p (i j) -> p i j", j=SIDE)
-                for first in (0, SIDE // 2):
-                    middle, last = first + VECTOR_ROWS // 2, first + SIDE // 2
-                    finish_on_scalar(nc, result, scaled[m], row[m], middle, last)
-                    finish(nc, result, scaled[m], row[m], first, middle)
-                    nc.sync.dma_start(out=out[m * P : (m + 1) * P, first:last, :], in_=result[:, first:last, :])
+            finish_half(m, SIDE // 2)

from contextlib import ExitStack

import concourse.mybir as mybir
from concourse.masks import make_identity

FLOPS = 2 * 512 * 2048 * 2048 + 2 * 512 * 2048 * 1024

F32 = mybir.dt.float32
BF16 = mybir.dt.bfloat16
I32 = mybir.dt.int32
U8 = mybir.dt.uint8
FP8X4 = mybir.dt.float8_e4m3fn_x4
ALU = mybir.AluOpType
ACT = mybir.ActivationFunctionType
AXIS = mybir.AxisListType

P = 128
PACK = 4
K_PASS = P * PACK
HID = 2048
PASSES = HID // K_PASS
TOKENS = 512
TOKEN_TILES = TOKENS // P
SIDE = 32
DOUT = SIDE * SIDE
N_TILE = 512
SLOPE = 0.01
EPS = 1e-8
Z_LINEAR = 30.0
EARLY_GROUPS = 5
ROUNDS = 10
BLOCK_ROWS = P // SIDE
VECTOR_ENDS = (8, 12, 18)
VECTOR_ROWS = VECTOR_ENDS[-1]
BLOCK_ORDER = (0, 1, 5, 2, 6, 3, 4, 7)
FOLD_REPEAT = 2
CLOCK_START = 4
CLOCK_RUN = 6
CLOCK_COLUMNS = 80


def load_scale_planes(nc, keep, scales, n_cols, name):
    planes = keep.tile([P, n_cols], U8, name=name, align_bytes=64)
    nc.vector.memset(planes[:].bitcast(I32), 0)
    for quadrant in range(4):
        nc.sync.dma_start(
            out=planes[32 * quadrant : 32 * quadrant + 16, :].bitcast(I32),
            in_=scales[:, 4 * quadrant : 4 * quadrant + 4, :].bitcast(I32),
        )
    return planes


def load_words(nc, codes, words, c, first, last):
    by_partition = words.rearrange("g p n t -> g p (n t)").bitcast(I32).rearrange("g p n -> p g n")
    nc.sync.dma_start(out=codes[:, first:last, :], in_=by_partition[:, first:last, c * N_TILE : (c + 1) * N_TILE])


def flip_two_passes(nc, psum, ident, words, g, grouped, copy):
    flipped = psum.tile([P, N_TILE], F32, name="flipped", tag="bank")[:].rearrange("p (g u r) -> p g u r", g=2, u=2)
    for i in range(2):
        for u in range(2):
            start = 256 * (g + i) + u
            nc.tensor.transpose(flipped[:, i, u, :], words[:, start : start + 255 : 2], ident[:])
    copy(
        out=grouped[:, g : g + 2, :, :].rearrange("p g r t -> p (g r t)").bitcast(F32).rearrange("p (g r u) -> p g r u", g=2, u=2),
        in_=flipped.rearrange("p g u r -> p g r u"),
    )


def quantise(nc, grouped, codes, planes):
    nc.vector.quantize_mx(out=codes.bitcast(FP8X4), scales=planes, in_=grouped.rearrange("p r t -> p (r t)"))


def fit_channels(nc, fitted, raw):
    nc.vector.tensor_copy(
        out=fitted.rearrange("p (t o i) -> p o t i", t=PACK, i=4), in_=raw.rearrange("p (o i t) -> p o t i", t=PACK, i=4)
    )


def scale_rows(nc, scaled, mat, factor, first, last):
    nc.vector.tensor_tensor(
        out=scaled[:, first:last, :],
        in0=mat[:, first:last, :],
        in1=factor[:, first:last].unsqueeze(2).to_broadcast([P, last - first, SIDE]),
        op=ALU.mult,
    )


def scale_rows_on_scalar(nc, scaled, mat, factor, first, last):
    for x in range(first, last):
        nc.scalar.activation(out=scaled[:, x, :], in_=mat[:, x, :], func=ACT.Copy, scale=factor[:, x : x + 1])


def turn_over(copy, mat_t, mat):
    copy(
        out=mat_t[:].rearrange("p j (b i) -> p b j i", i=BLOCK_ROWS), in_=mat[:].rearrange("p (b i) j -> p b j i", i=BLOCK_ROWS)
    )


def finish(nc, result, mat_t, factor, first, last):
    nc.vector.tensor_tensor(
        out=result[:, first:last, :].rearrange("p i (b j) -> p b i j", j=BLOCK_ROWS),
        in0=mat_t[:, :, first:last].rearrange("p (b j) i -> p b i j", j=BLOCK_ROWS),
        in1=factor[:, first:last].unsqueeze(1).unsqueeze(3).to_broadcast([P, SIDE // BLOCK_ROWS, last - first, BLOCK_ROWS]),
        op=ALU.mult,
    )


def finish_on_scalar(nc, result, mat_t, factor, first, last):
    for i in range(first, last):
        nc.scalar.activation(out=result[:, i, :], in_=mat_t[:, :, i], func=ACT.Copy, scale=factor[:, i : i + 1])


def add_up(nc, sums, ident, scaled):
    for b in BLOCK_ORDER:
        nc.tensor.matmul(
            out=sums,
            lhsT=scaled[:, b * BLOCK_ROWS : (b + 1) * BLOCK_ROWS, :].rearrange("p x y -> p (x y)"),
            rhs=ident[:],
            is_transpose=True,
            start=(b == BLOCK_ORDER[0]),
            stop=(b == BLOCK_ORDER[-1]),
        )


def tile_matchingnet_pa_kernel(tc, h3, W4_words, W4_scales, b4, W5_words, W5_scales, b5, out):
    nc = tc.nc
    with ExitStack() as stack:
        keep = stack.enter_context(tc.tile_pool(name="keep", bufs=1))
        work = stack.enter_context(tc.tile_pool(name="work", bufs=2))
        small = stack.enter_context(tc.tile_pool(name="small", bufs=4))

        stack.enter_context(tc.manual_schedule())

        x_rows = keep.tile([P, TOKEN_TILES, HID], BF16, name="x_rows")
        for m in range(TOKEN_TILES):
            nc.sync.dma_start(out=x_rows[:, m, :], in_=h3[m * P : (m + 1) * P, :])
            if m == 0:
                w4_raw_planes = load_scale_planes(nc, keep, W4_scales, HID, "w4_raw_planes")
        w4_raw = [keep.tile([P, PASSES, N_TILE], I32, name="w4_raw%d" % c) for c in range(PASSES)]
        for c in range(PASSES):
            for g in range(0, PASSES, 2):
                load_words(nc, w4_raw[c], W4_words, c, g, g + 2)
        w5_planes = load_scale_planes(nc, keep, W5_scales, DOUT, "w5_planes")
        w5_codes = [keep.tile([P, PASSES, N_TILE], I32, name="w5_codes%d" % c, align_bytes=64) for c in range(DOUT // N_TILE)]
        for c in range(DOUT // N_TILE):
            load_words(nc, w5_codes[c], W5_words, c, 0, PASSES)
        b5_all = keep.tile([P, DOUT], BF16, name="b5_all")
        nc.sync.dma_start(out=b5_all[:], in_=b5.partition_broadcast(P))
        b4_raw = keep.tile([P, PASSES, PACK], BF16, name="b4_raw")
        nc.scalar.dma_start(out=b4_raw[:], in_=b4.rearrange("(c p t) -> p c t", p=P, t=PACK))
        b4_col = keep.tile([P, PASSES, PACK], F32, name="b4_col")

        ident = keep.tile([P, P], F32, name="ident")
        make_identity(nc, ident[:])
        fold = keep.tile([P, FOLD_REPEAT, SIDE], F32, name="fold")
        nc.vector.tensor_reduce(
            out=fold[:, 0, :], in_=ident[:].rearrange("p (x y) -> p y x", x=BLOCK_ROWS), axis=AXIS.X, op=ALU.add
        )
        nc.vector.tensor_copy(out=fold[:, 1:, :], in_=fold[:, 0:1, :].to_broadcast([P, FOLD_REPEAT - 1, SIDE]))
        one = keep.tile([P, 1], F32, name="one")
        nc.vector.memset(one[:], 1.0)

        w4_codes = [keep.tile([P, PASSES, N_TILE], I32, name="w4_codes%d" % c, align_bytes=64) for c in range(PASSES)]
        w4_planes = keep.tile([P, HID], U8, name="w4_planes", align_bytes=64)
        nc.vector.tensor_copy(out=b4_col[:], in_=b4_raw[:])

        x_codes = keep.tile([P, PASSES, TOKENS], I32, name="x_codes", align_bytes=64)
        x_planes = keep.tile([P, PASSES, TOKENS], U8, name="x_planes", align_bytes=64)
        h_codes = keep.tile([P, PASSES, TOKENS], I32, name="h_codes", align_bytes=64)
        h_planes = keep.tile([P, PASSES, TOKENS], U8, name="h_planes", align_bytes=64)
        z = keep.tile([P, TOKEN_TILES, DOUT], F32, name="z")
        kern = [keep.tile([P, SIDE, SIDE], F32, name="kern%d" % m) for m in range(TOKEN_TILES)]

        with tc.psum_pool(name="psum", bufs=8) as psum:

            clock_start = psum.tile([P, N_TILE], F32, name="clock_start", tag="bank")
            for i in range(CLOCK_START):
                nc.tensor.matmul(out=clock_start[:, 0:P], lhsT=ident[:], rhs=ident[:], start=True, stop=True)

            def quantise_x(m, g):
                toks = slice(m * P, (m + 1) * P)
                quantise(nc, x_grouped[m][:, g, :, :], x_codes[:, g, toks], x_planes[:, g, toks])

            def fit_w4(c, g):
                fit_channels(nc, w4_codes[c][:, g, :], w4_raw[c][:, g, :])

            def fit_w4_planes(c):
                cols = slice(c * N_TILE, (c + 1) * N_TILE)
                nc.vector.tensor_copy(
                    out=w4_planes[:, cols].rearrange("p (t m) -> p t m", t=PACK),
                    in_=w4_raw_planes[:, cols].rearrange("p (m t) -> p t m", t=PACK),
                )

            fit_w4_planes(0)
            x_grouped = []
            for m in range(TOKEN_TILES):
                x_grouped.append(work.tile([P, PASSES, P, PACK], BF16, name="x_grouped", tag="x_grouped", align_bytes=64))
                words = x_rows[:, m, :].bitcast(F32)
                flip_two_passes(nc, psum, ident, words, 0, x_grouped[m], nc.scalar.copy)
                if m > 0:
                    for g in range(PASSES):
                        quantise_x(m - 1, g)
                flip_two_passes(nc, psum, ident, words, 2, x_grouped[m], nc.vector.tensor_copy if m % 2 else nc.scalar.copy)
            for g in range(PASSES):
                fit_w4(0, g)
                quantise_x(TOKEN_TILES - 1, g)

            def layer_1(c):
                pre = work.tile([P, PACK, TOKENS], F32, tag="pre")
                for t in range(PACK):
                    acc = psum.tile([P, N_TILE], F32, name="acc", tag="bank")
                    for g in range(PASSES):
                        nc.tensor.matmul_mx(
                            out=acc[:],
                            lhsT=w4_codes[c][:, g, t * P : (t + 1) * P].bitcast(FP8X4),
                            lhsT_scale=w4_planes[4 * g : P, c * N_TILE + t * P : c * N_TILE + (t + 1) * P],
                            rhs=x_codes[:, g, :].bitcast(FP8X4),
                            rhs_scale=x_planes[:, g, :],
                            start=(g == 0),
                            stop=(g == PASSES - 1),
                        )
                    nc.scalar.activation(out=pre[:, t, :], in_=acc[:], func=ACT.Identity, bias=b4_col[:, c, t : t + 1])
                halves = []
                for toks in (slice(0, TOKENS // 2), slice(TOKENS // 2, TOKENS)):
                    grouped = work.tile([P, TOKENS // 2, PACK], BF16, tag="h_grouped", bufs=4, align_bytes=64)
                    side_by_side = pre[:, :, toks].rearrange("p t r -> p r t")
                    nc.vector.scalar_tensor_tensor(
                        out=grouped[:], in0=side_by_side, scalar=SLOPE, in1=side_by_side, op0=ALU.mult, op1=ALU.max
                    )
                    halves.append((grouped, toks))
                for grouped, toks in halves:
                    quantise(nc, grouped[:], h_codes[:, c, toks], h_planes[:, c, toks])

            def layer_2(m, c, acc, first, last):
                for g in range(first, last):
                    nc.tensor.matmul_mx(
                        out=acc[:],
                        lhsT=h_codes[:, g, m * P : (m + 1) * P].bitcast(FP8X4),
                        lhsT_scale=h_planes[:, g, m * P : (m + 1) * P],
                        rhs=w5_codes[c][:, g, :].bitcast(FP8X4),
                        rhs_scale=w5_planes[4 * g : P, c * N_TILE : (c + 1) * N_TILE],
                        start=(g == 0),
                        stop=(g == PASSES - 1),
                    )

            def fit_w4_chunk(c):
                fit_w4_planes(c)
                for g in range(PASSES):
                    fit_w4(c, g)

            fit_w4_chunk(1)
            fit_w4_chunk(2)
            layer_1(0)
            fit_w4_chunk(3)
            for c in range(1, PASSES):
                layer_1(c)

            groups = [(m, c) for m in range(TOKEN_TILES) for c in range(DOUT // N_TILE)]
            accs = []
            for m, c in groups[:EARLY_GROUPS]:
                accs.append(psum.tile([P, N_TILE], F32, name="acc", tag="bank"))
                layer_2(m, c, accs[-1], 0, PASSES - 1)

            def exponential(m, c):
                cols = slice(c * N_TILE, (c + 1) * N_TILE)
                part = kern[m][:].rearrange("p i j -> p (i j)")[:, cols]
                nc.vector.tensor_scalar(out=part, in0=z[:, m, cols], scalar1=Z_LINEAR, scalar2=None, op0=ALU.min)
                nc.scalar.activation(out=part, in_=part, func=ACT.Exp)

            for k, (m, c) in enumerate(groups):
                if k < EARLY_GROUPS:
                    layer_2(m, c, accs[k], PASSES - 1, PASSES)
                else:
                    accs.append(psum.tile([P, N_TILE], F32, name="acc", tag="bank"))
                    layer_2(m, c, accs[k], 0, PASSES)
                cols = slice(c * N_TILE, (c + 1) * N_TILE)
                nc.vector.tensor_tensor(out=z[:, m, cols], in0=accs[k][:], in1=b5_all[:, cols], op=ALU.add)
                if k > 0:
                    exponential(*groups[k - 1])
            exponential(*groups[-1])

            clock_run = psum.tile([P, N_TILE], F32, name="clock_run", tag="bank")
            for m, c in groups[:CLOCK_RUN]:
                cols = slice(c * N_TILE, (c + 1) * N_TILE)
                nc.tensor.matmul(out=clock_run[:], lhsT=ident[:], rhs=z[:, m, cols], start=True, stop=True)

        psum_clock = stack.enter_context(tc.psum_pool(name="psum_clock", bufs=1))
        clock = psum_clock.tile([P, N_TILE], F32, name="clock")
        psum_sums = stack.enter_context(tc.psum_pool(name="psum_sums", bufs=4))
        psum_back = stack.enter_context(tc.psum_pool(name="psum_back", bufs=3))
        kern_t = [keep.tile([P, SIDE, SIDE], F32, name="kern_t%d" % m) for m in range(TOKEN_TILES)]
        scaled = [keep.tile([P, SIDE, SIDE], F32, name="scaled%d" % m) for m in range(TOKEN_TILES)]
        row = [keep.tile([P, SIDE], F32, name="row%d" % m) for m in range(TOKEN_TILES)]
        col = [keep.tile([P, SIDE], F32, name="col%d" % m) for m in range(TOKEN_TILES)]
        for m in range(TOKEN_TILES):
            nc.vector.memset(row[m][:], 1.0)
            nc.vector.memset(col[m][:], 1.0)

        steps = []
        for it in range(ROUNDS):
            steps.extend((m, kern[m], row[m], col[m]) for m in range(TOKEN_TILES))
            steps.extend((m, kern_t[m], col[m], row[m]) for m in range(TOKEN_TILES))
        sums = {}
        back = {}
        inverse = {}

        def add_up_step(n, product):
            sums[n] = psum_sums.tile([P, N_TILE], F32, name="sums", tag="sums")[:, 0:P]
            add_up(nc, sums[n], ident, product)

        def fold_step(n):
            sums_sb = small.tile([P, P], F32, name="sums_sb", tag="sums_sb")
            nc.scalar.copy(out=sums_sb[:], in_=sums[n])
            back[n] = psum_back.tile([P, N_TILE], F32, name="back", tag="back")[:, 0 : FOLD_REPEAT * SIDE]
            nc.tensor.matmul(
                out=back[n],
                lhsT=sums_sb[:],
                rhs=fold[:].rearrange("p r y -> p (r y)"),
                start=True,
                stop=True,
            )

        def keep_clock(columns):
            nc.tensor.matmul(
                out=clock[:, 0:columns],
                lhsT=ident[:],
                rhs=ident[:, 0:columns],
                start=True,
                stop=True,
            )

        def invert_step(n):
            inverse[n] = small.tile([P, SIDE], F32, name="inverse", tag="inverse")
            nc.vector.reciprocal(out=inverse[n][:], in_=back[n][:, 0:SIDE])

        def renew_step(n):
            renewed = steps[n][3]
            nc.vector.scalar_tensor_tensor(
                out=renewed[:], in0=renewed[:], scalar=1.0 / EPS, in1=inverse[n][:], op0=ALU.mult, op1=ALU.min
            )

        for m in range(TOKEN_TILES):
            log = kern[m][:].rearrange("p i j -> p (i j)")
            nc.scalar.activation(out=log, in_=log, func=ACT.Ln, bias=one[:])
            if m == TOKEN_TILES - 1:
                fold_step(0)
                fold_step(1)
            nc.vector.tensor_tensor(out=log, in0=z[:, m, :], in1=log, op=ALU.max)
            add_up_step(m, kern[m])
            keep_clock(P)
        turn_over(nc.scalar.copy, kern_t[0], kern[0])
        turn_over(nc.scalar.copy, kern_t[1], kern[1])
        invert_step(0)
        renew_step(0)

        starts = (0,) + VECTOR_ENDS[:-1]
        for n in range(TOKEN_TILES, len(steps)):
            fold_step(n - 2)
            keep_clock(P if n < 3 * TOKEN_TILES else CLOCK_COLUMNS)
            invert_step(n - 3)
            m, mat, factor = steps[n][0:3]
            scale_rows_on_scalar(nc, scaled[m], mat, factor, VECTOR_ROWS, SIDE)
            scale_rows(nc, scaled[m], mat, factor, starts[0], VECTOR_ENDS[0])
            renew_step(n - 3)
            for first, last in zip(starts[1:], VECTOR_ENDS[1:]):
                scale_rows(nc, scaled[m], mat, factor, first, last)
            add_up_step(n, scaled[m])
            if n - 2 in (2, 3):
                turn_over(nc.vector.tensor_copy, kern_t[n - 2], kern[n - 2])

        def finish_half(m, first):
            result = z[:, m, :].rearrange("p (i j) -> p i j", j=SIDE)
            middle, last = first + VECTOR_ROWS // 2, first + SIDE // 2
            finish_on_scalar(nc, result, scaled[m], row[m], middle, last)
            finish(nc, result, scaled[m], row[m], first, middle)
            nc.sync.dma_start(out=out[m * P : (m + 1) * P, first:last, :], in_=result[:, first:last, :])

        for m in range(TOKEN_TILES):
            n = len(steps) + m
            if n - 2 < len(steps):
                fold_step(n - 2)
            finish_half(m, 0)
            if n - 3 < len(steps):
                invert_step(n - 3)
                renew_step(n - 3)
            finish_half(m, SIDE // 2)
